import numpy as np
import ml_dtypes


def mxq(x, axis, fmt="e4m3"):
    dtype, down = {"e4m3": (ml_dtypes.float8_e4m3fn, 7), "e5m2": (ml_dtypes.float8_e5m2, 14)}[fmt]
    v = np.moveaxis(np.asarray(x, np.float32).astype(ml_dtypes.bfloat16).astype(np.float64), axis, -1)
    blocks = v.reshape(v.shape[:-1] + (-1, 32))
    amax = np.abs(blocks).max(-1, keepdims=True)
    byte = np.maximum(np.where(amax > 0, np.frexp(amax)[1] - 1 + 127, 0) - down, 1)
    scale = np.exp2(byte - 127.0)
    codes = (blocks / scale).astype(np.float32).astype(dtype).astype(np.float64)
    return np.moveaxis((codes * scale).reshape(v.shape), -1, axis)


WIDE = False


def mx_kscale(k):
    if not WIDE:
        return np.ones(k)
    levels = np.array([10, -10, 5, -5, 0])
    if k % 512:
        return np.exp2(np.random.permutation(np.resize(levels, k // 32))).repeat(32)
    a = np.empty((k // 512, 16))
    for p in range(k // 512):
        a[p, :8] = np.random.permutation(np.resize(levels, 8))
        for g in range(8):
            far = levels[np.abs(levels - a[p, g]) >= 10]
            a[p, g + 8] = far[np.random.randint(len(far))]
    return np.exp2(a.ravel()).repeat(32)


BF16 = ml_dtypes.bfloat16


def bf(x):
    return np.asarray(x, np.float32).astype(BF16)


def f64(x):
    return np.asarray(x).astype(np.float64)


B, S, D, R = 2, 1024, 1024, 8
EPS = 1e-6


def setup_inputs():
    s, t = mx_kscale(D), mx_kscale(D)
    return {"x": bf(np.random.standard_normal((B, S, D)) * s),
            "pos_emb": bf(np.random.standard_normal((1, S, D)) * s),
            "enc_w0": bf(np.random.standard_normal((D, D)) / np.sqrt(D) / s[None, :] * t[:, None]),
            "enc_w1": bf(np.random.standard_normal((D, D)) / np.sqrt(D) / t[None, :])}


def reference(x, pos_emb, enc_w0, enc_w1):
    x = f64(x)
    y = x + f64(pos_emb)[:, : x.shape[1]]
    h = np.maximum(mxq(y, 2, "e4m3") @ mxq(f64(enc_w0), 1, "e4m3").T, 0.0)
    h = np.maximum(mxq(h, 2, "e4m3") @ mxq(f64(enc_w1), 1, "e4m3").T, 0.0)
    return h / (np.sqrt((h * h).sum(-1, keepdims=True)) + EPS)

@@ -1,0 +1,272 @@
+from contextlib import ExitStack
+
+import concourse.mybir as mybir
+from concourse.masks import make_identity
+
+BF16 = mybir.dt.bfloat16
+F32 = mybir.dt.float32
+U32 = mybir.dt.uint32
+U8 = mybir.dt.uint8
+FP8X4 = mybir.dt.float8_e4m3fn_x4
+ACT = mybir.ActivationFunctionType
+ALU = mybir.AluOpType
+
+P = 128
+D = 1024
+TOKENS = 2048
+POSITIONS = 1024
+PACK = 4
+PASSES = D // (P * PACK)
+WORD_TILES = D // 2 // P
+PAIR = 2
+ROUND = PAIR * P
+ROUNDS = TOKENS // ROUND
+POS_ROUNDS = POSITIONS // ROUND
+HALF = 512
+HALVES = D // HALF
+EPS = 1e-6
+
+FLOPS = 2 * 2 * TOKENS * D * D
+
+
+def tile_mybadtransfomerblock_pa_kernel(tc, x, pos_emb, enc_w0, enc_w1, out):
+    nc = tc.nc
+
+    x_rounds = x.flatten_outer_dims().rearrange("(r p i) d -> r p i d", p=P, i=PAIR)
+    pos_rounds = pos_emb.flatten_outer_dims().rearrange("(r p i) d -> r p i d", p=P, i=PAIR)
+    out_rounds = out.flatten_outer_dims().rearrange("(r p i) d -> r p i d", p=P, i=PAIR)
+    w0_quads = enc_w0.rearrange("(q p t) k -> q p t k", p=P, t=PACK)
+    w0_pairs = [
+        w0_quads[a // 2][:, PAIR * (a % 2) : PAIR * (a % 2 + 1), :] for a in range(D // ROUND)
+    ]
+    w1_pairs = enc_w1.rearrange("(a e p) k -> a p e k", p=P, e=PAIR)
+
+    with ExitStack() as ctx:
+        const = ctx.enter_context(tc.tile_pool(name="const", bufs=1))
+        raw = ctx.enter_context(tc.tile_pool(name="raw", bufs=1))
+        keep = ctx.enter_context(tc.tile_pool(name="keep", bufs=1))
+        two = ctx.enter_context(tc.tile_pool(name="two", bufs=2))
+        three = ctx.enter_context(tc.tile_pool(name="three", bufs=3))
+        four = ctx.enter_context(tc.tile_pool(name="four", bufs=4))
+        psum = ctx.enter_context(tc.psum_pool(name="psum", bufs=8))
+        ctx.enter_context(tc.manual_schedule())
+
+        warm = const.tile([P, 1], F32)
+        nc.vector.memset(warm[:], 1.0)
+        nc.scalar.sqrt(warm[:], warm[:])
+
+        ident = const.tile([P, P], F32)
+        make_identity(nc, ident[:])
+
+        def load(name, source):
+            rows = raw.tile([P, PAIR, D], BF16, name=name)
+            nc.sync.dma_start(out=rows[:], in_=source)
+            return rows
+
+        x_sb = {}
+        pos_sb = {}
+        x_sb[0] = load("x_sb0", x_rounds[0])
+        pos_sb[0] = load("pos_sb0", pos_rounds[0])
+        w0_sb = [load("w0_sb%d" % a, w0_pairs[a]) for a in range(D // ROUND)]
+        x_sb[1] = load("x_sb1", x_rounds[1])
+        pos_sb[1] = load("pos_sb1", pos_rounds[1])
+        w1_sb = [load("w1_sb%d" % a, w1_pairs[a]) for a in range(D // ROUND)]
+        for r in range(2, ROUNDS):
+            x_sb[r] = load("x_sb%d" % r, x_rounds[r])
+            if r < POS_ROUNDS:
+                pos_sb[r] = load("pos_sb%d" % r, pos_rounds[r])
+
+        def transpose_rows(rows, copy_out, grouped_words):
+            bank = psum.tile([P, WORD_TILES, P], F32, tag="bank")
+            words = rows.bitcast(F32)
+            for c in range(WORD_TILES):
+                first = 2 * P * (c // 2) + c % 2
+                last = 2 * P * (c // 2 + 1)
+                nc.tensor.transpose(bank[:, c, :], words[:, first:last:2], ident[:])
+            copy_out(out=grouped_words, in_=bank[:].rearrange("p (g u) c -> p g c u", u=2))
+
+        def quantise(grouped, codes, scales):
+            nc.vector.quantize_mx(
+                out=codes[:].rearrange("p g c -> p (g c)").bitcast(FP8X4),
+                scales=scales[:].rearrange("p g c -> p (g c)"),
+                in_=grouped[:].rearrange("p g c t -> p (g c t)"),
+            )
+
+        def prepare_weight(name, pairs):
+            codes = []
+            scales = []
+            for h in range(HALVES):
+                w_grouped = two.tile([P, PASSES, HALF, PACK], BF16, align_bytes=64)
+                w_words = w_grouped[:].bitcast(F32)
+                for j in range(HALF // P):
+                    copy_out = nc.scalar.copy if j % 2 == 0 else nc.vector.tensor_copy
+                    transpose_rows(
+                        pairs[(HALF // ROUND) * h + j // PAIR][:, j % PAIR, :],
+                        copy_out,
+                        w_words[:, :, j * P : (j + 1) * P, :],
+                    )
+                w_codes = keep.tile(
+                    [P, PASSES, HALF], U32, name="%s_codes%d" % (name, h), align_bytes=64
+                )
+                w_scales = keep.tile(
+                    [P, PASSES, HALF], U8, name="%s_scales%d" % (name, h), align_bytes=64
+                )
+                quantise(w_grouped, w_codes, w_scales)
+                codes.append(w_codes)
+                scales.append(w_scales)
+            return codes, scales
+
+        x_grouped = {}
+        pos_grouped = {}
+        sum_squares = {}
+        y_grouped = {}
+        y_codes = {}
+        y_scales = {}
+        h1_grouped = {}
+        h1_codes = {}
+        h1_scales = {}
+        h2 = {}
+        norm = {}
+
+        def transpose_inputs(r):
+            x_g = two.tile([P, PASSES, ROUND, PACK], BF16, name="x_g")
+            for i in range(PAIR):
+                transpose_rows(
+                    x_sb[r][:, i, :],
+                    nc.scalar.copy if i == 0 else nc.vector.tensor_copy,
+                    x_g[:].bitcast(F32)[:, :, i * P : (i + 1) * P, :],
+                )
+            x_grouped[r] = x_g
+            if r < POS_ROUNDS:
+                pos_g = keep.tile([P, PASSES, ROUND, PACK], BF16, name="pos_g%d" % r)
+                for i in range(PAIR):
+                    transpose_rows(
+                        pos_sb[r][:, i, :],
+                        nc.scalar.copy,
+                        pos_g[:].bitcast(F32)[:, :, i * P : (i + 1) * P, :],
+                    )
+                pos_grouped[r] = pos_g
+
+        def add_positions(r):
+            y_g = two.tile([P, PASSES, ROUND, PACK], BF16, name="y_g", align_bytes=64)
+            nc.vector.tensor_tensor(
+                out=y_g[:].rearrange("p g c t -> p (g c t)"),
+                in0=x_grouped[r][:].rearrange("p g c t -> p (g c t)"),
+                in1=pos_grouped[r % POS_ROUNDS][:].rearrange("p g c t -> p (g c t)"),
+                op=ALU.add,
+            )
+            y_grouped[r] = y_g
+
+        def quantise_y(r):
+            y_c = three.tile([P, PASSES, ROUND], U32, name="y_c", align_bytes=64)
+            y_s = three.tile([P, PASSES, ROUND], U8, name="y_s", align_bytes=64)
+            quantise(y_grouped[r], y_c, y_s)
+            y_codes[r] = y_c
+            y_scales[r] = y_s
+
+        def layer_one(r):
+            h1_g = two.tile([P, PASSES, ROUND, PACK], BF16, name="h1_g", align_bytes=64)
+            for q in range(HALVES):
+                for i in range(PAIR):
+                    bank = psum.tile([P, PACK, P], F32, tag="bank")
+                    for t in range(PACK):
+                        for g in range(PASSES):
+                            nc.tensor.matmul_mx(
+                                out=bank[:, t, :],
+                                lhsT=w0_codes[q][:, g, t * P : (t + 1) * P].bitcast(FP8X4),
+                                lhsT_scale=w0_scales[q][:, g, t * P : (t + 1) * P],
+                                rhs=y_codes[r][:, g, i * P : (i + 1) * P].bitcast(FP8X4),
+                                rhs_scale=y_scales[r][:, g, i * P : (i + 1) * P],
+                                start=(g == 0),
+                                stop=(g == PASSES - 1),
+                            )
+                    nc.scalar.activation(
+                        out=h1_g[:, q, i * P : (i + 1) * P, :],
+                        in_=bank[:].rearrange("p t c -> p c t"),
+                        func=ACT.Relu,
+                    )
+            h1_grouped[r] = h1_g
+
+        def quantise_h1(r):
+            h1_c = three.tile([P, PASSES, ROUND], U32, name="h1_c", align_bytes=64)
+            h1_s = three.tile([P, PASSES, ROUND], U8, name="h1_s", align_bytes=64)
+            quantise(h1_grouped[r], h1_c, h1_s)
+            h1_codes[r] = h1_c
+            h1_scales[r] = h1_s
+
+        def layer_two(r):
+            h2_r = four.tile([P, PAIR, D], F32, name="h2_r")
+            for i in range(PAIR):
+                for n in range(HALVES):
+                    bank = psum.tile([P, HALF], F32, tag="bank")
+                    for g in range(PASSES):
+                        nc.tensor.matmul_mx(
+                            out=bank[:],
+                            lhsT=h1_codes[r][:, g, i * P : (i + 1) * P].bitcast(FP8X4),
+                            lhsT_scale=h1_scales[r][:, g, i * P : (i + 1) * P],
+                            rhs=w1_codes[n][:, g, :].bitcast(FP8X4),
+                            rhs_scale=w1_scales[n][:, g, :],
+                            start=(g == 0),
+                            stop=(g == PASSES - 1),
+                        )
+                    nc.vector.tensor_scalar_max(
+                        out=h2_r[:, i, n * HALF : (n + 1) * HALF], in0=bank[:], scalar1=0.0
+                    )
+            h2[r] = h2_r
+
+        def square(r, i):
+            if i == 0:
+                sum_sq = four.tile([P, PAIR], F32, name="sum_sq")
+                sum_squares[r] = sum_sq
+            squares = two.tile([P, D], BF16, name="squares")
+            nc.scalar.activation(
+                out=squares[:],
+                in_=h2[r][:, i, :],
+                func=ACT.Square,
+                accum_out=sum_squares[r][:, i : i + 1],
+            )
+
+        def take_root(r):
+            norm_r = four.tile([P, PAIR], F32, name="norm_r")
+            nc.scalar.sqrt(norm_r[:], sum_squares[r][:])
+            norm[r] = norm_r
+
+        def normalise(r):
+            inverse = four.tile([P, PAIR], F32, name="inverse")
+            nc.vector.tensor_scalar_add(out=inverse[:], in0=norm[r][:], scalar1=EPS)
+            nc.vector.reciprocal(out=inverse[:], in_=inverse[:])
+            scaler = nc.vector if r == ROUNDS - 1 else nc.gpsimd
+            for i in range(PAIR):
+                scaler.tensor_scalar(
+                    out=h2[r][:, i, :],
+                    in0=h2[r][:, i, :],
+                    scalar1=inverse[:, i : i + 1],
+                    scalar2=0.0,
+                    op0=ALU.mult,
+                    op1=ALU.add,
+                )
+                nc.sync.dma_start(out=out_rounds[r][:, i, :], in_=h2[r][:, i, :])
+
+        for s in range(ROUNDS + 4):
+            if s < ROUNDS:
+                transpose_inputs(s)
+            if 0 <= s - 2 < ROUNDS:
+                quantise_h1(s - 2)
+            if s < ROUNDS:
+                add_positions(s)
+            if 0 <= s - 4:
+                normalise(s - 4)
+            if s < ROUNDS:
+                quantise_y(s)
+            if s == 0:
+                w0_codes, w0_scales = prepare_weight("w0", w0_sb)
+            if 0 <= s - 1 < ROUNDS:
+                layer_one(s - 1)
+            if 0 <= s - 3 < ROUNDS:
+                square(s - 3, 0)
+                square(s - 3, 1)
+                take_root(s - 3)
+            if s == 1:
+                w1_codes, w1_scales = prepare_weight("w1", w1_sb)
+            if 0 <= s - 2 < ROUNDS:
+                layer_two(s - 2)

@@ -16,8 +16,8 @@ D = 1024
 TOKENS = 2048
 POSITIONS = 1024
 PACK = 4
-PASSES = D // (P * PACK)
-WORD_TILES = D // 2 // P
+K_PASS = P * PACK
+PASSES = D // K_PASS
 PAIR = 2
 ROUND = PAIR * P
 ROUNDS = TOKENS // ROUND
@@ -35,11 +35,8 @@ def tile_mybadtransfomerblock_pa_kernel(tc, x, pos_emb, enc_w0, enc_w1, out):
     x_rounds = x.flatten_outer_dims().rearrange("(r p i) d -> r p i d", p=P, i=PAIR)
     pos_rounds = pos_emb.flatten_outer_dims().rearrange("(r p i) d -> r p i d", p=P, i=PAIR)
     out_rounds = out.flatten_outer_dims().rearrange("(r p i) d -> r p i d", p=P, i=PAIR)
-    w0_quads = enc_w0.rearrange("(q p t) k -> q p t k", p=P, t=PACK)
-    w0_pairs = [
-        w0_quads[a // 2][:, PAIR * (a % 2) : PAIR * (a % 2 + 1), :] for a in range(D // ROUND)
-    ]
-    w1_pairs = enc_w1.rearrange("(a e p) k -> a p e k", p=P, e=PAIR)
+    w0_halves = enc_w0.rearrange("(h p j) k -> h p j k", p=P, j=PACK)
+    w1_halves = enc_w1.rearrange("(h j p) k -> h p j k", p=P, j=PACK)
 
     with ExitStack() as ctx:
         const = ctx.enter_context(tc.tile_pool(name="const", bufs=1))
@@ -58,32 +55,36 @@ def tile_mybadtransfomerblock_pa_kernel(tc, x, pos_emb, enc_w0, enc_w1, out):
         ident = const.tile([P, P], F32)
         make_identity(nc, ident[:])
 
-        def load(name, source):
-            rows = raw.tile([P, PAIR, D], BF16, name=name)
-            nc.sync.dma_start(out=rows[:], in_=source)
-            return rows
-
         x_sb = {}
         pos_sb = {}
-        x_sb[0] = load("x_sb0", x_rounds[0])
-        pos_sb[0] = load("pos_sb0", pos_rounds[0])
-        w0_sb = [load("w0_sb%d" % a, w0_pairs[a]) for a in range(D // ROUND)]
-        x_sb[1] = load("x_sb1", x_rounds[1])
-        pos_sb[1] = load("pos_sb1", pos_rounds[1])
-        w1_sb = [load("w1_sb%d" % a, w1_pairs[a]) for a in range(D // ROUND)]
-        for r in range(2, ROUNDS):
-            x_sb[r] = load("x_sb%d" % r, x_rounds[r])
-            if r < POS_ROUNDS:
-                pos_sb[r] = load("pos_sb%d" % r, pos_rounds[r])
 
-        def transpose_rows(rows, copy_out, grouped_words):
-            bank = psum.tile([P, WORD_TILES, P], F32, tag="bank")
-            words = rows.bitcast(F32)
-            for c in range(WORD_TILES):
-                first = 2 * P * (c // 2) + c % 2
-                last = 2 * P * (c // 2 + 1)
-                nc.tensor.transpose(bank[:, c, :], words[:, first:last:2], ident[:])
-            copy_out(out=grouped_words, in_=bank[:].rearrange("p (g u) c -> p g c u", u=2))
+        def load_round(r):
+            rows = raw.tile([P, PAIR, D], BF16, name="x_sb%d" % r)
+            nc.sync.dma_start(out=rows[:], in_=x_rounds[r])
+            x_sb[r] = rows
+            if r < POS_ROUNDS:
+                rows = raw.tile([P, PAIR, D], BF16, name="pos_sb%d" % r)
+                nc.sync.dma_start(out=rows[:], in_=pos_rounds[r])
+                pos_sb[r] = rows
+
+        def load_weight(name, halves, h):
+            parts = []
+            for c in range(2):
+                rows = raw.tile([P, PAIR, D], BF16, name="%s_sb%d%d" % (name, h, c))
+                nc.sync.dma_start(out=rows[:], in_=halves[h][:, PAIR * c : PAIR * (c + 1), :])
+                parts.append(rows)
+            return parts
+
+        w0_sb = {}
+        w1_sb = {}
+        load_round(0)
+        w0_sb[0] = load_weight("w0", w0_halves, 0)
+        w0_sb[1] = load_weight("w0", w0_halves, 1)
+        w1_sb[0] = load_weight("w1", w1_halves, 0)
+        load_round(1)
+        w1_sb[1] = load_weight("w1", w1_halves, 1)
+        for r in range(2, ROUNDS):
+            load_round(r)
 
         def quantise(grouped, codes, scales):
             nc.vector.quantize_mx(
@@ -92,33 +93,54 @@ def tile_mybadtransfomerblock_pa_kernel(tc, x, pos_emb, enc_w0, enc_w1, out):
                 in_=grouped[:].rearrange("p g c t -> p (g c t)"),
             )
 
-        def prepare_weight(name, pairs):
-            codes = []
-            scales = []
-            for h in range(HALVES):
-                w_grouped = two.tile([P, PASSES, HALF, PACK], BF16, align_bytes=64)
-                w_words = w_grouped[:].bitcast(F32)
-                for j in range(HALF // P):
-                    copy_out = nc.scalar.copy if j % 2 == 0 else nc.vector.tensor_copy
-                    transpose_rows(
-                        pairs[(HALF // ROUND) * h + j // PAIR][:, j % PAIR, :],
-                        copy_out,
-                        w_words[:, :, j * P : (j + 1) * P, :],
-                    )
-                w_codes = keep.tile(
-                    [P, PASSES, HALF], U32, name="%s_codes%d" % (name, h), align_bytes=64
-                )
-                w_scales = keep.tile(
-                    [P, PASSES, HALF], U8, name="%s_scales%d" % (name, h), align_bytes=64
-                )
-                quantise(w_grouped, w_codes, w_scales)
-                codes.append(w_codes)
-                scales.append(w_scales)
-            return codes, scales
+        codes_of = {}
+        scales_of = {}
 
-        x_grouped = {}
-        pos_grouped = {}
-        sum_squares = {}
+        grouped_of = {}
+
+        def transpose_weight(sb, grouped, h, c, first, engines):
+            w_words = grouped[:].bitcast(F32)
+            for e in range(PAIR):
+                words = sb[h][c][:, e, :].bitcast(F32)
+                bank = psum.tile([P, 2 * PASSES, P], F32, tag="bank")
+                for g in range(PASSES):
+                    for u in range(2):
+                        nc.tensor.transpose(
+                            bank[:, 2 * g + u, :],
+                            words[:, 2 * P * g + u : 2 * P * (g + 1) : 2],
+                            ident[:],
+                        )
+                engines[e](
+                    out=w_words[:, :, first + e * P : first + (e + 1) * P, :],
+                    in_=bank[:].rearrange("p (g u) c -> p g c u", u=2),
+                )
+
+        def transpose_w0(h, c, engines):
+            w0_grouped = three.tile([P, PASSES, ROUND, PACK], BF16, name="w0_grouped", align_bytes=64)
+            grouped_of["w0", h, c] = w0_grouped
+            transpose_weight(w0_sb, w0_grouped, h, c, 0, engines)
+
+        def quantise_w0(h, c):
+            w_codes = keep.tile([P, PASSES, ROUND], U32, name="w0_codes%d%d" % (h, c), align_bytes=64)
+            w_scales = keep.tile([P, PASSES, ROUND], U8, name="w0_scales%d%d" % (h, c), align_bytes=64)
+            quantise(grouped_of["w0", h, c], w_codes, w_scales)
+            codes_of["w0", h, c] = w_codes
+            scales_of["w0", h, c] = w_scales
+
+        def transpose_w1(h, c, engines):
+            if c == 0:
+                w1_grouped = two.tile([P, PASSES, HALF, PACK], BF16, name="w1_grouped", align_bytes=64)
+                grouped_of["w1", h] = w1_grouped
+            transpose_weight(w1_sb, grouped_of["w1", h], h, c, ROUND * c, engines)
+
+        def quantise_w1(h):
+            w_codes = keep.tile([P, PASSES, HALF], U32, name="w1_codes%d" % h, align_bytes=64)
+            w_scales = keep.tile([P, PASSES, HALF], U8, name="w1_scales%d" % h, align_bytes=64)
+            quantise(grouped_of["w1", h], w_codes, w_scales)
+            codes_of["w1", h] = w_codes
+            scales_of["w1", h] = w_scales
+
+        y_rows = {}
         y_grouped = {}
         y_codes = {}
         y_scales = {}
@@ -126,35 +148,32 @@ def tile_mybadtransfomerblock_pa_kernel(tc, x, pos_emb, enc_w0, enc_w1, out):
         h1_codes = {}
         h1_scales = {}
         h2 = {}
+        sum_squares = {}
         norm = {}
 
-        def transpose_inputs(r):
-            x_g = two.tile([P, PASSES, ROUND, PACK], BF16, name="x_g")
-            for i in range(PAIR):
-                transpose_rows(
-                    x_sb[r][:, i, :],
-                    nc.scalar.copy if i == 0 else nc.vector.tensor_copy,
-                    x_g[:].bitcast(F32)[:, :, i * P : (i + 1) * P, :],
-                )
-            x_grouped[r] = x_g
-            if r < POS_ROUNDS:
-                pos_g = keep.tile([P, PASSES, ROUND, PACK], BF16, name="pos_g%d" % r)
-                for i in range(PAIR):
-                    transpose_rows(
-                        pos_sb[r][:, i, :],
-                        nc.scalar.copy,
-                        pos_g[:].bitcast(F32)[:, :, i * P : (i + 1) * P, :],
-                    )
-                pos_grouped[r] = pos_g
-
         def add_positions(r):
+            y = two.tile([P, PAIR, D], BF16, name="y_rows")
+            pos = pos_sb[r % POS_ROUNDS]
+            for u in range(2):
+                nc.vector.tensor_tensor(
+                    out=y[:].rearrange("p i (g u w e) -> p (i g) u w e", g=PASSES, u=2, e=2)[:, :, u],
+                    in0=x_sb[r][:].rearrange("p i (g w u e) -> p (i g) u w e", u=2, w=P, e=2)[:, :, u],
+                    in1=pos[:].rearrange("p i (g w u e) -> p (i g) u w e", u=2, w=P, e=2)[:, :, u],
+                    op=ALU.add,
+                )
+            y_rows[r] = y
+
+        def transpose_y(r):
             y_g = two.tile([P, PASSES, ROUND, PACK], BF16, name="y_g", align_bytes=64)
-            nc.vector.tensor_tensor(
-                out=y_g[:].rearrange("p g c t -> p (g c t)"),
-                in0=x_grouped[r][:].rearrange("p g c t -> p (g c t)"),
-                in1=pos_grouped[r % POS_ROUNDS][:].rearrange("p g c t -> p (g c t)"),
-                op=ALU.add,
-            )
+            for i in range(PAIR):
+                words = y_rows[r][:, i, :].bitcast(F32)
+                bank = psum.tile([P, 2 * PASSES, P], F32, tag="bank")
+                for c in range(2 * PASSES):
+                    nc.tensor.transpose(bank[:, c, :], words[:, c * P : (c + 1) * P], ident[:])
+                y_engines[i](
+                    out=y_g[:].bitcast(F32)[:, :, i * P : (i + 1) * P, :],
+                    in_=bank[:].rearrange("p (g u) c -> p g c u", u=2),
+                )
             y_grouped[r] = y_g
 
         def quantise_y(r):
@@ -164,28 +183,31 @@ def tile_mybadtransfomerblock_pa_kernel(tc, x, pos_emb, enc_w0, enc_w1, out):
             y_codes[r] = y_c
             y_scales[r] = y_s
 
-        def layer_one(r):
-            h1_g = two.tile([P, PASSES, ROUND, PACK], BF16, name="h1_g", align_bytes=64)
-            for q in range(HALVES):
-                for i in range(PAIR):
-                    bank = psum.tile([P, PACK, P], F32, tag="bank")
-                    for t in range(PACK):
-                        for g in range(PASSES):
-                            nc.tensor.matmul_mx(
-                                out=bank[:, t, :],
-                                lhsT=w0_codes[q][:, g, t * P : (t + 1) * P].bitcast(FP8X4),
-                                lhsT_scale=w0_scales[q][:, g, t * P : (t + 1) * P],
-                                rhs=y_codes[r][:, g, i * P : (i + 1) * P].bitcast(FP8X4),
-                                rhs_scale=y_scales[r][:, g, i * P : (i + 1) * P],
-                                start=(g == 0),
-                                stop=(g == PASSES - 1),
-                            )
-                    nc.scalar.activation(
-                        out=h1_g[:, q, i * P : (i + 1) * P, :],
-                        in_=bank[:].rearrange("p t c -> p c t"),
-                        func=ACT.Relu,
-                    )
-            h1_grouped[r] = h1_g
+        def layer_one(r, q):
+            if q == 0:
+                h1_g = two.tile([P, PASSES, ROUND, PACK], BF16, name="h1_g", align_bytes=64)
+                h1_grouped[r] = h1_g
+            for i in range(PAIR):
+                bank = psum.tile([P, PACK, P], F32, tag="bank")
+                for t in range(PACK):
+                    w_codes = codes_of["w0", q, t // PAIR]
+                    w_scales = scales_of["w0", q, t // PAIR]
+                    features = slice(t % PAIR * P, (t % PAIR + 1) * P)
+                    for g in range(PASSES):
+                        nc.tensor.matmul_mx(
+                            out=bank[:, t, :],
+                            lhsT=w_codes[:, g, features].bitcast(FP8X4),
+                            lhsT_scale=w_scales[:, g, features],
+                            rhs=y_codes[r][:, g, i * P : (i + 1) * P].bitcast(FP8X4),
+                            rhs_scale=y_scales[r][:, g, i * P : (i + 1) * P],
+                            start=(g == 0),
+                            stop=(g == PASSES - 1),
+                        )
+                nc.scalar.activation(
+                    out=h1_grouped[r][:, q, i * P : (i + 1) * P, :],
+                    in_=bank[:].rearrange("p t c -> p c t"),
+                    func=ACT.Relu,
+                )
 
         def quantise_h1(r):
             h1_c = three.tile([P, PASSES, ROUND], U32, name="h1_c", align_bytes=64)
@@ -194,79 +216,119 @@ def tile_mybadtransfomerblock_pa_kernel(tc, x, pos_emb, enc_w0, enc_w1, out):
             h1_codes[r] = h1_c
             h1_scales[r] = h1_s
 
-        def layer_two(r):
-            h2_r = four.tile([P, PAIR, D], F32, name="h2_r")
-            for i in range(PAIR):
-                for n in range(HALVES):
-                    bank = psum.tile([P, HALF], F32, tag="bank")
-                    for g in range(PASSES):
-                        nc.tensor.matmul_mx(
-                            out=bank[:],
-                            lhsT=h1_codes[r][:, g, i * P : (i + 1) * P].bitcast(FP8X4),
-                            lhsT_scale=h1_scales[r][:, g, i * P : (i + 1) * P],
-                            rhs=w1_codes[n][:, g, :].bitcast(FP8X4),
-                            rhs_scale=w1_scales[n][:, g, :],
-                            start=(g == 0),
-                            stop=(g == PASSES - 1),
-                        )
-                    nc.vector.tensor_scalar_max(
-                        out=h2_r[:, i, n * HALF : (n + 1) * HALF], in0=bank[:], scalar1=0.0
-                    )
-            h2[r] = h2_r
-
-        def square(r, i):
+        def layer_two(r, i, engines):
             if i == 0:
-                sum_sq = four.tile([P, PAIR], F32, name="sum_sq")
-                sum_squares[r] = sum_sq
-            squares = two.tile([P, D], BF16, name="squares")
-            nc.scalar.activation(
-                out=squares[:],
-                in_=h2[r][:, i, :],
-                func=ACT.Square,
-                accum_out=sum_squares[r][:, i : i + 1],
-            )
+                h2_r = four.tile([P, PAIR, D], F32, name="h2_r")
+                h2[r] = h2_r
+            for n in range(HALVES):
+                bank = psum.tile([P, HALF], F32, tag="bank")
+                for g in range(PASSES):
+                    nc.tensor.matmul_mx(
+                        out=bank[:],
+                        lhsT=h1_codes[r][:, g, i * P : (i + 1) * P].bitcast(FP8X4),
+                        lhsT_scale=h1_scales[r][:, g, i * P : (i + 1) * P],
+                        rhs=codes_of["w1", n][:, g, :].bitcast(FP8X4),
+                        rhs_scale=scales_of["w1", n][:, g, :],
+                        start=(g == 0),
+                        stop=(g == PASSES - 1),
+                    )
+                h2_half = h2[r][:, i, n * HALF : (n + 1) * HALF]
+                if engines[n] == "vector":
+                    nc.vector.tensor_scalar_max(out=h2_half, in0=bank[:], scalar1=0.0)
+                else:
+                    nc.scalar.activation(out=h2_half, in_=bank[:], func=ACT.Relu)
 
-        def take_root(r):
-            norm_r = four.tile([P, PAIR], F32, name="norm_r")
-            nc.scalar.sqrt(norm_r[:], sum_squares[r][:])
-            norm[r] = norm_r
+        def take_norms(tiles):
+            sum_sq = four.tile([P, PAIR], F32, name="sum_sq")
+            for c, (r, i) in enumerate(tiles):
+                squares = two.tile([P, D], BF16, name="squares")
+                nc.scalar.activation(
+                    out=squares[:],
+                    in_=h2[r][:, i, :],
+                    func=ACT.Square,
+                    accum_out=sum_sq[:, c : c + 1],
+                )
+            norm_t = four.tile([P, PAIR], F32, name="norm_t")
+            nc.scalar.sqrt(norm_t[:, : len(tiles)], sum_sq[:, : len(tiles)])
+            norm[tiles] = norm_t
 
-        def normalise(r):
+        def invert_norms(tiles):
             inverse = four.tile([P, PAIR], F32, name="inverse")
-            nc.vector.tensor_scalar_add(out=inverse[:], in0=norm[r][:], scalar1=EPS)
-            nc.vector.reciprocal(out=inverse[:], in_=inverse[:])
-            scaler = nc.vector if r == ROUNDS - 1 else nc.gpsimd
-            for i in range(PAIR):
-                scaler.tensor_scalar(
+            some = inverse[:, : len(tiles)]
+            nc.vector.tensor_scalar_add(out=some, in0=norm[tiles][:, : len(tiles)], scalar1=EPS)
+            nc.vector.reciprocal(out=some, in_=some)
+            inverses[tiles] = inverse
+
+        def scale(tiles, engine):
+            for c, (r, i) in enumerate(tiles):
+                engine.tensor_scalar(
                     out=h2[r][:, i, :],
                     in0=h2[r][:, i, :],
-                    scalar1=inverse[:, i : i + 1],
+                    scalar1=inverses[tiles][:, c : c + 1],
                     scalar2=0.0,
                     op0=ALU.mult,
                     op1=ALU.add,
                 )
                 nc.sync.dma_start(out=out_rounds[r][:, i, :], in_=h2[r][:, i, :])
 
-        for s in range(ROUNDS + 4):
+        inverses = {}
+        scalar_copy = nc.scalar.copy
+        vector_copy = nc.vector.tensor_copy
+        both = (scalar_copy, vector_copy)
+        scalar_only = (scalar_copy, scalar_copy)
+        y_engines = both
+        on_vector = ("vector", "vector")
+
+        add_positions(0)
+        transpose_y(0)
+        transpose_w0(0, 0, both)
+        quantise_y(0)
+        quantise_w0(0, 0)
+        transpose_w0(0, 1, both)
+        transpose_w0(1, 0, both)
+        quantise_w0(0, 1)
+        transpose_w0(1, 1, both)
+        quantise_w0(1, 0)
+        layer_one(0, 0)
+        quantise_w0(1, 1)
+        transpose_w1(0, 0, both)
+        transpose_w1(0, 1, both)
+        layer_one(0, 1)
+        add_positions(1)
+        quantise_w1(0)
+        transpose_y(1)
+        quantise_y(1)
+        transpose_w1(1, 0, scalar_only)
+        transpose_w1(1, 1, scalar_only)
+        quantise_h1(0)
+        add_positions(2)
+        quantise_w1(1)
+
+        groups = {0: ((0, 0),), ROUNDS: ((ROUNDS - 1, 1),)}
+        for k in range(1, ROUNDS):
+            groups[k] = ((k - 1, 1), (k, 0))
+
+        for s in range(2, ROUNDS + 2):
+            k = s - 2
             if s < ROUNDS:
-                transpose_inputs(s)
-            if 0 <= s - 2 < ROUNDS:
-                quantise_h1(s - 2)
-            if s < ROUNDS:
-                add_positions(s)
-            if 0 <= s - 4:
-                normalise(s - 4)
+                transpose_y(s)
+            if s - 1 < ROUNDS:
+                layer_one(s - 1, 0)
+                layer_one(s - 1, 1)
+            if s + 1 < ROUNDS:
+                add_positions(s + 1)
             if s < ROUNDS:
                 quantise_y(s)
-            if s == 0:
-                w0_codes, w0_scales = prepare_weight("w0", w0_sb)
-            if 0 <= s - 1 < ROUNDS:
-                layer_one(s - 1)
-            if 0 <= s - 3 < ROUNDS:
-                square(s - 3, 0)
-                square(s - 3, 1)
-                take_root(s - 3)
-            if s == 1:
-                w1_codes, w1_scales = prepare_weight("w1", w1_sb)
-            if 0 <= s - 2 < ROUNDS:
-                layer_two(s - 2)
+            if 1 <= k:
+                invert_norms(groups[k - 1])
+                scale(groups[k - 1], nc.gpsimd)
+            layer_two(k, 0, on_vector)
+            if s - 1 < ROUNDS:
+                quantise_h1(s - 1)
+            take_norms(groups[k])
+            layer_two(k, 1, on_vector)
+        invert_norms(groups[ROUNDS - 1])
+        scale(groups[ROUNDS - 1], nc.vector)
+        take_norms(groups[ROUNDS])
+        invert_norms(groups[ROUNDS])
+        scale(groups[ROUNDS], nc.vector)

@@ -55,36 +55,31 @@ def tile_mybadtransfomerblock_pa_kernel(tc, x, pos_emb, enc_w0, enc_w1, out):
         ident = const.tile([P, P], F32)
         make_identity(nc, ident[:])
 
+        def load(name, source):
+            rows = raw.tile([P, PAIR, D], BF16, name=name)
+            nc.sync.dma_start(out=rows[:], in_=source)
+            return rows
+
         x_sb = {}
         pos_sb = {}
-
-        def load_round(r):
-            rows = raw.tile([P, PAIR, D], BF16, name="x_sb%d" % r)
-            nc.sync.dma_start(out=rows[:], in_=x_rounds[r])
-            x_sb[r] = rows
-            if r < POS_ROUNDS:
-                rows = raw.tile([P, PAIR, D], BF16, name="pos_sb%d" % r)
-                nc.sync.dma_start(out=rows[:], in_=pos_rounds[r])
-                pos_sb[r] = rows
-
-        def load_weight(name, halves, h):
-            parts = []
-            for c in range(2):
-                rows = raw.tile([P, PAIR, D], BF16, name="%s_sb%d%d" % (name, h, c))
-                nc.sync.dma_start(out=rows[:], in_=halves[h][:, PAIR * c : PAIR * (c + 1), :])
-                parts.append(rows)
-            return parts
-
         w0_sb = {}
         w1_sb = {}
-        load_round(0)
-        w0_sb[0] = load_weight("w0", w0_halves, 0)
-        w0_sb[1] = load_weight("w0", w0_halves, 1)
-        w1_sb[0] = load_weight("w1", w1_halves, 0)
-        load_round(1)
-        w1_sb[1] = load_weight("w1", w1_halves, 1)
+        w0_sb[0, 0] = load("w0_sb00", w0_halves[0][:, 0:2, :])
+        x_sb[0] = load("x_sb0", x_rounds[0])
+        pos_sb[0] = load("pos_sb0", pos_rounds[0])
+        w0_sb[0, 1] = load("w0_sb01", w0_halves[0][:, 2:4, :])
+        w0_sb[1, 0] = load("w0_sb10", w0_halves[1][:, 0:2, :])
+        w0_sb[1, 1] = load("w0_sb11", w0_halves[1][:, 2:4, :])
+        w1_sb[0, 0] = load("w1_sb00", w1_halves[0][:, 0:2, :])
+        w1_sb[0, 1] = load("w1_sb01", w1_halves[0][:, 2:4, :])
+        x_sb[1] = load("x_sb1", x_rounds[1])
+        pos_sb[1] = load("pos_sb1", pos_rounds[1])
+        w1_sb[1, 0] = load("w1_sb10", w1_halves[1][:, 0:2, :])
+        w1_sb[1, 1] = load("w1_sb11", w1_halves[1][:, 2:4, :])
         for r in range(2, ROUNDS):
-            load_round(r)
+            x_sb[r] = load("x_sb%d" % r, x_rounds[r])
+            if r < POS_ROUNDS:
+                pos_sb[r] = load("pos_sb%d" % r, pos_rounds[r])
 
         def quantise(grouped, codes, scales):
             nc.vector.quantize_mx(
@@ -101,7 +96,7 @@ def tile_mybadtransfomerblock_pa_kernel(tc, x, pos_emb, enc_w0, enc_w1, out):
         def transpose_weight(sb, grouped, h, c, first, engines):
             w_words = grouped[:].bitcast(F32)
             for e in range(PAIR):
-                words = sb[h][c][:, e, :].bitcast(F32)
+                words = sb[h, c][:, e, :].bitcast(F32)
                 bank = psum.tile([P, 2 * PASSES, P], F32, tag="bank")
                 for g in range(PASSES):
                     for u in range(2):
@@ -152,15 +147,13 @@ def tile_mybadtransfomerblock_pa_kernel(tc, x, pos_emb, enc_w0, enc_w1, out):
         norm = {}
 
         def add_positions(r):
-            y = two.tile([P, PAIR, D], BF16, name="y_rows")
-            pos = pos_sb[r % POS_ROUNDS]
-            for u in range(2):
-                nc.vector.tensor_tensor(
-                    out=y[:].rearrange("p i (g u w e) -> p (i g) u w e", g=PASSES, u=2, e=2)[:, :, u],
-                    in0=x_sb[r][:].rearrange("p i (g w u e) -> p (i g) u w e", u=2, w=P, e=2)[:, :, u],
-                    in1=pos[:].rearrange("p i (g w u e) -> p (i g) u w e", u=2, w=P, e=2)[:, :, u],
-                    op=ALU.add,
-                )
+            y = three.tile([P, PAIR, D], BF16, name="y_rows")
+            nc.vector.tensor_tensor(
+                out=y[:].rearrange("p i d -> p (i d)"),
+                in0=x_sb[r][:].rearrange("p i d -> p (i d)"),
+                in1=pos_sb[r % POS_ROUNDS][:].rearrange("p i d -> p (i d)"),
+                op=ALU.add,
+            )
             y_rows[r] = y
 
         def transpose_y(r):
@@ -168,8 +161,13 @@ def tile_mybadtransfomerblock_pa_kernel(tc, x, pos_emb, enc_w0, enc_w1, out):
             for i in range(PAIR):
                 words = y_rows[r][:, i, :].bitcast(F32)
                 bank = psum.tile([P, 2 * PASSES, P], F32, tag="bank")
-                for c in range(2 * PASSES):
-                    nc.tensor.transpose(bank[:, c, :], words[:, c * P : (c + 1) * P], ident[:])
+                for g in range(PASSES):
+                    for u in range(2):
+                        nc.tensor.transpose(
+                            bank[:, 2 * g + u, :],
+                            words[:, 2 * P * g + u : 2 * P * (g + 1) : 2],
+                            ident[:],
+                        )
                 y_engines[i](
                     out=y_g[:].bitcast(F32)[:, :, i * P : (i + 1) * P, :],
                     in_=bank[:].rearrange("p (g u) c -> p g c u", u=2),
@@ -279,20 +277,20 @@ def tile_mybadtransfomerblock_pa_kernel(tc, x, pos_emb, enc_w0, enc_w1, out):
         y_engines = both
         on_vector = ("vector", "vector")
 
-        add_positions(0)
-        transpose_y(0)
         transpose_w0(0, 0, both)
-        quantise_y(0)
+        add_positions(0)
         quantise_w0(0, 0)
+        transpose_y(0)
         transpose_w0(0, 1, both)
+        quantise_y(0)
         transpose_w0(1, 0, both)
         quantise_w0(0, 1)
         transpose_w0(1, 1, both)
         quantise_w0(1, 0)
         layer_one(0, 0)
         quantise_w0(1, 1)
-        transpose_w1(0, 0, both)
-        transpose_w1(0, 1, both)
+        transpose_w1(0, 0, scalar_only)
+        transpose_w1(0, 1, scalar_only)
         layer_one(0, 1)
         add_positions(1)
         quantise_w1(0)
@@ -300,8 +298,8 @@ def tile_mybadtransfomerblock_pa_kernel(tc, x, pos_emb, enc_w0, enc_w1, out):
         quantise_y(1)
         transpose_w1(1, 0, scalar_only)
         transpose_w1(1, 1, scalar_only)
-        quantise_h1(0)
         add_positions(2)
+        quantise_h1(0)
         quantise_w1(1)
 
         groups = {0: ((0, 0),), ROUNDS: ((ROUNDS - 1, 1),)}

@@ -24,6 +24,8 @@ ROUNDS = TOKENS // ROUND
 POS_ROUNDS = POSITIONS // ROUND
 HALF = 512
 HALVES = D // HALF
+HALF_BLOCK = 16
+BLOCKS = K_PASS // (2 * HALF_BLOCK)
 EPS = 1e-6
 
 FLOPS = 2 * 2 * TOKENS * D * D
@@ -93,27 +95,32 @@ def tile_mybadtransfomerblock_pa_kernel(tc, x, pos_emb, enc_w0, enc_w1, out):
 
         grouped_of = {}
 
-        def transpose_weight(sb, grouped, h, c, first, engines):
-            w_words = grouped[:].bitcast(F32)
-            for e in range(PAIR):
-                words = sb[h, c][:, e, :].bitcast(F32)
-                bank = psum.tile([P, 2 * PASSES, P], F32, tag="bank")
-                for g in range(PASSES):
-                    for u in range(2):
-                        nc.tensor.transpose(
-                            bank[:, 2 * g + u, :],
-                            words[:, 2 * P * g + u : 2 * P * (g + 1) : 2],
-                            ident[:],
-                        )
-                engines[e](
-                    out=w_words[:, :, first + e * P : first + (e + 1) * P, :],
-                    in_=bank[:].rearrange("p (g u) c -> p g c u", u=2),
-                )
+        def blocks(rows):
+            return rows[:].rearrange("p i (g b u n) -> p (i g) u b n", u=2, b=BLOCKS, n=HALF_BLOCK)
+
+        def halved(rows):
+            return rows[:].rearrange("p i (g u b n) -> p (i g) u b n", u=2, b=BLOCKS, n=HALF_BLOCK)
+
+        w0_rows = {}
+
+        def halve_w0(h, c):
+            w_rows = three.tile([P, PAIR, D], BF16, name="w_rows")
+            for u in range(2):
+                nc.vector.tensor_copy(out=halved(w_rows)[:, :, u], in_=blocks(w0_sb[h, c])[:, :, u])
+            w0_rows[h, c] = w_rows
 
         def transpose_w0(h, c, engines):
             w0_grouped = three.tile([P, PASSES, ROUND, PACK], BF16, name="w0_grouped", align_bytes=64)
             grouped_of["w0", h, c] = w0_grouped
-            transpose_weight(w0_sb, w0_grouped, h, c, 0, engines)
+            for e in range(PAIR):
+                words = w0_rows[h, c][:, e, :].bitcast(F32)
+                bank = psum.tile([P, 2 * PASSES, P], F32, tag="bank")
+                for k in range(2 * PASSES):
+                    nc.tensor.transpose(bank[:, k, :], words[:, k * P : (k + 1) * P], ident[:])
+                engines[e](
+                    out=w0_grouped[:].bitcast(F32)[:, :, e * P : (e + 1) * P, :],
+                    in_=bank[:].rearrange("p (g u) c -> p g c u", u=2),
+                )
 
         def quantise_w0(h, c):
             w_codes = keep.tile([P, PASSES, ROUND], U32, name="w0_codes%d%d" % (h, c), align_bytes=64)
@@ -126,7 +133,21 @@ def tile_mybadtransfomerblock_pa_kernel(tc, x, pos_emb, enc_w0, enc_w1, out):
             if c == 0:
                 w1_grouped = two.tile([P, PASSES, HALF, PACK], BF16, name="w1_grouped", align_bytes=64)
                 grouped_of["w1", h] = w1_grouped
-            transpose_weight(w1_sb, grouped_of["w1", h], h, c, ROUND * c, engines)
+            for e in range(PAIR):
+                j = PAIR * c + e
+                words = w1_sb[h, c][:, e, :].bitcast(F32)
+                bank = psum.tile([P, 2 * PASSES, P], F32, tag="bank")
+                for g in range(PASSES):
+                    for u in range(2):
+                        nc.tensor.transpose(
+                            bank[:, 2 * g + u, :],
+                            words[:, 2 * P * g + u : 2 * P * (g + 1) : 2],
+                            ident[:],
+                        )
+                engines[e](
+                    out=grouped_of["w1", h][:].bitcast(F32)[:, :, j * P : (j + 1) * P, :],
+                    in_=bank[:].rearrange("p (g u) c -> p g c u", u=2),
+                )
 
         def quantise_w1(h):
             w_codes = keep.tile([P, PASSES, HALF], U32, name="w1_codes%d" % h, align_bytes=64)
@@ -148,12 +169,13 @@ def tile_mybadtransfomerblock_pa_kernel(tc, x, pos_emb, enc_w0, enc_w1, out):
 
         def add_positions(r):
             y = three.tile([P, PAIR, D], BF16, name="y_rows")
-            nc.vector.tensor_tensor(
-                out=y[:].rearrange("p i d -> p (i d)"),
-                in0=x_sb[r][:].rearrange("p i d -> p (i d)"),
-                in1=pos_sb[r % POS_ROUNDS][:].rearrange("p i d -> p (i d)"),
-                op=ALU.add,
-            )
+            for u in range(2):
+                nc.vector.tensor_tensor(
+                    out=halved(y)[:, :, u],
+                    in0=blocks(x_sb[r])[:, :, u],
+                    in1=blocks(pos_sb[r % POS_ROUNDS])[:, :, u],
+                    op=ALU.add,
+                )
             y_rows[r] = y
 
         def transpose_y(r):
@@ -161,13 +183,8 @@ def tile_mybadtransfomerblock_pa_kernel(tc, x, pos_emb, enc_w0, enc_w1, out):
             for i in range(PAIR):
                 words = y_rows[r][:, i, :].bitcast(F32)
                 bank = psum.tile([P, 2 * PASSES, P], F32, tag="bank")
-                for g in range(PASSES):
-                    for u in range(2):
-                        nc.tensor.transpose(
-                            bank[:, 2 * g + u, :],
-                            words[:, 2 * P * g + u : 2 * P * (g + 1) : 2],
-                            ident[:],
-                        )
+                for c in range(2 * PASSES):
+                    nc.tensor.transpose(bank[:, c, :], words[:, c * P : (c + 1) * P], ident[:])
                 y_engines[i](
                     out=y_g[:].bitcast(F32)[:, :, i * P : (i + 1) * P, :],
                     in_=bank[:].rearrange("p (g u) c -> p g c u", u=2),
@@ -277,28 +294,32 @@ def tile_mybadtransfomerblock_pa_kernel(tc, x, pos_emb, enc_w0, enc_w1, out):
         y_engines = both
         on_vector = ("vector", "vector")
 
-        transpose_w0(0, 0, both)
+        halve_w0(0, 0)
+        transpose_w0(0, 0, scalar_only)
         add_positions(0)
         quantise_w0(0, 0)
         transpose_y(0)
-        transpose_w0(0, 1, both)
+        halve_w0(0, 1)
+        transpose_w0(0, 1, scalar_only)
+        halve_w0(1, 0)
+        transpose_w0(1, 0, scalar_only)
         quantise_y(0)
-        transpose_w0(1, 0, both)
+        halve_w0(1, 1)
         quantise_w0(0, 1)
-        transpose_w0(1, 1, both)
+        transpose_w0(1, 1, scalar_only)
         quantise_w0(1, 0)
         layer_one(0, 0)
         quantise_w0(1, 1)
+        add_positions(1)
         transpose_w1(0, 0, scalar_only)
         transpose_w1(0, 1, scalar_only)
         layer_one(0, 1)
-        add_positions(1)
         quantise_w1(0)
         transpose_y(1)
+        add_positions(2)
         quantise_y(1)
         transpose_w1(1, 0, scalar_only)
         transpose_w1(1, 1, scalar_only)
-        add_positions(2)
         quantise_h1(0)
         quantise_w1(1)
 

@@ -22,6 +22,7 @@ PAIR = 2
 ROUND = PAIR * P
 ROUNDS = TOKENS // ROUND
 POS_ROUNDS = POSITIONS // ROUND
+BATCH = ROUNDS // POS_ROUNDS
 HALF = 512
 HALVES = D // HALF
 HALF_BLOCK = 16
@@ -62,26 +63,28 @@ def tile_mybadtransfomerblock_pa_kernel(tc, x, pos_emb, enc_w0, enc_w1, out):
             nc.sync.dma_start(out=rows[:], in_=source)
             return rows
 
+        def token_round(r):
+            return r % BATCH * POS_ROUNDS + r // BATCH
+
         x_sb = {}
         pos_sb = {}
         w0_sb = {}
         w1_sb = {}
         w0_sb[0, 0] = load("w0_sb00", w0_halves[0][:, 0:2, :])
-        x_sb[0] = load("x_sb0", x_rounds[0])
+        x_sb[0] = load("x_sb0", x_rounds[token_round(0)])
         pos_sb[0] = load("pos_sb0", pos_rounds[0])
         w0_sb[0, 1] = load("w0_sb01", w0_halves[0][:, 2:4, :])
         w0_sb[1, 0] = load("w0_sb10", w0_halves[1][:, 0:2, :])
         w0_sb[1, 1] = load("w0_sb11", w0_halves[1][:, 2:4, :])
         w1_sb[0, 0] = load("w1_sb00", w1_halves[0][:, 0:2, :])
         w1_sb[0, 1] = load("w1_sb01", w1_halves[0][:, 2:4, :])
-        x_sb[1] = load("x_sb1", x_rounds[1])
-        pos_sb[1] = load("pos_sb1", pos_rounds[1])
+        x_sb[1] = load("x_sb1", x_rounds[token_round(1)])
         w1_sb[1, 0] = load("w1_sb10", w1_halves[1][:, 0:2, :])
         w1_sb[1, 1] = load("w1_sb11", w1_halves[1][:, 2:4, :])
         for r in range(2, ROUNDS):
-            x_sb[r] = load("x_sb%d" % r, x_rounds[r])
-            if r < POS_ROUNDS:
-                pos_sb[r] = load("pos_sb%d" % r, pos_rounds[r])
+            if r % BATCH == 0:
+                pos_sb[r // BATCH] = load("pos_sb%d" % (r // BATCH), pos_rounds[r // BATCH])
+            x_sb[r] = load("x_sb%d" % r, x_rounds[token_round(r)])
 
         def quantise(grouped, codes, scales):
             nc.vector.quantize_mx(
@@ -109,18 +112,20 @@ def tile_mybadtransfomerblock_pa_kernel(tc, x, pos_emb, enc_w0, enc_w1, out):
                 nc.vector.tensor_copy(out=halved(w_rows)[:, :, u], in_=blocks(w0_sb[h, c])[:, :, u])
             w0_rows[h, c] = w_rows
 
+        def transpose_halved(words, grouped, i, copy_out):
+            bank = psum.tile([P, 2 * PASSES, P], F32, tag="bank")
+            for c in range(2 * PASSES):
+                nc.tensor.transpose(bank[:, c, :], words[:, c * P : (c + 1) * P], ident[:])
+            copy_out(
+                out=grouped.bitcast(F32)[:, :, i * P : (i + 1) * P, :],
+                in_=bank[:].rearrange("p (g u) c -> p g c u", u=2),
+            )
+
         def transpose_w0(h, c, engines):
             w0_grouped = three.tile([P, PASSES, ROUND, PACK], BF16, name="w0_grouped", align_bytes=64)
             grouped_of["w0", h, c] = w0_grouped
             for e in range(PAIR):
-                words = w0_rows[h, c][:, e, :].bitcast(F32)
-                bank = psum.tile([P, 2 * PASSES, P], F32, tag="bank")
-                for k in range(2 * PASSES):
-                    nc.tensor.transpose(bank[:, k, :], words[:, k * P : (k + 1) * P], ident[:])
-                engines[e](
-                    out=w0_grouped[:].bitcast(F32)[:, :, e * P : (e + 1) * P, :],
-                    in_=bank[:].rearrange("p (g u) c -> p g c u", u=2),
-                )
+                transpose_halved(w0_rows[h, c][:, e, :].bitcast(F32), w0_grouped[:], e, engines[e])
 
         def quantise_w0(h, c):
             w_codes = keep.tile([P, PASSES, ROUND], U32, name="w0_codes%d%d" % (h, c), align_bytes=64)
@@ -157,51 +162,46 @@ def tile_mybadtransfomerblock_pa_kernel(tc, x, pos_emb, enc_w0, enc_w1, out):
             scales_of["w1", h] = w_scales
 
         y_rows = {}
-        y_grouped = {}
-        y_codes = {}
-        y_scales = {}
-        h1_grouped = {}
-        h1_codes = {}
-        h1_scales = {}
+        grouped = {}
+        codes = {}
+        scales = {}
         h2 = {}
-        sum_squares = {}
-        norm = {}
+        sums = {}
+        norms = {}
+        inverses = {}
 
-        def add_positions(r):
+        def new_grouped(kind, r):
+            values = three.tile(
+                [P, PASSES, ROUND, PACK], BF16, name="%s_grouped" % kind, align_bytes=64
+            )
+            grouped[kind, r] = values
+
+        def quantise_round(kind, r):
+            packed = three.tile([P, PASSES, ROUND], U32, name="%s_codes" % kind, align_bytes=64)
+            bytes_of = three.tile([P, PASSES, ROUND], U8, name="%s_scales" % kind, align_bytes=64)
+            quantise(grouped[kind, r], packed, bytes_of)
+            codes[kind, r] = packed
+            scales[kind, r] = bytes_of
+
+        def add_positions(r, engines):
             y = three.tile([P, PAIR, D], BF16, name="y_rows")
             for u in range(2):
-                nc.vector.tensor_tensor(
+                engines[u].tensor_tensor(
                     out=halved(y)[:, :, u],
                     in0=blocks(x_sb[r])[:, :, u],
-                    in1=blocks(pos_sb[r % POS_ROUNDS])[:, :, u],
+                    in1=blocks(pos_sb[r // BATCH])[:, :, u],
                     op=ALU.add,
                 )
             y_rows[r] = y
 
-        def transpose_y(r):
-            y_g = two.tile([P, PASSES, ROUND, PACK], BF16, name="y_g", align_bytes=64)
+        def transpose_y(r, engines):
+            new_grouped("y", r)
             for i in range(PAIR):
-                words = y_rows[r][:, i, :].bitcast(F32)
-                bank = psum.tile([P, 2 * PASSES, P], F32, tag="bank")
-                for c in range(2 * PASSES):
-                    nc.tensor.transpose(bank[:, c, :], words[:, c * P : (c + 1) * P], ident[:])
-                y_engines[i](
-                    out=y_g[:].bitcast(F32)[:, :, i * P : (i + 1) * P, :],
-                    in_=bank[:].rearrange("p (g u) c -> p g c u", u=2),
-                )
-            y_grouped[r] = y_g
-
-        def quantise_y(r):
-            y_c = three.tile([P, PASSES, ROUND], U32, name="y_c", align_bytes=64)
-            y_s = three.tile([P, PASSES, ROUND], U8, name="y_s", align_bytes=64)
-            quantise(y_grouped[r], y_c, y_s)
-            y_codes[r] = y_c
-            y_scales[r] = y_s
+                transpose_halved(y_rows[r][:, i, :].bitcast(F32), grouped["y", r][:], i, engines[i])
 
         def layer_one(r, q):
             if q == 0:
-                h1_g = two.tile([P, PASSES, ROUND, PACK], BF16, name="h1_g", align_bytes=64)
-                h1_grouped[r] = h1_g
+                new_grouped("h1", r)
             for i in range(PAIR):
                 bank = psum.tile([P, PACK, P], F32, tag="bank")
                 for t in range(PACK):
@@ -213,23 +213,16 @@ def tile_mybadtransfomerblock_pa_kernel(tc, x, pos_emb, enc_w0, enc_w1, out):
                             out=bank[:, t, :],
                             lhsT=w_codes[:, g, features].bitcast(FP8X4),
                             lhsT_scale=w_scales[:, g, features],
-                            rhs=y_codes[r][:, g, i * P : (i + 1) * P].bitcast(FP8X4),
-                            rhs_scale=y_scales[r][:, g, i * P : (i + 1) * P],
+                            rhs=codes["y", r][:, g, i * P : (i + 1) * P].bitcast(FP8X4),
+                            rhs_scale=scales["y", r][:, g, i * P : (i + 1) * P],
                             start=(g == 0),
                             stop=(g == PASSES - 1),
                         )
                 nc.scalar.activation(
-                    out=h1_grouped[r][:, q, i * P : (i + 1) * P, :],
+                    out=grouped["h1", r][:, q, i * P : (i + 1) * P, :],
                     in_=bank[:].rearrange("p t c -> p c t"),
                     func=ACT.Relu,
                 )
-
-        def quantise_h1(r):
-            h1_c = three.tile([P, PASSES, ROUND], U32, name="h1_c", align_bytes=64)
-            h1_s = three.tile([P, PASSES, ROUND], U8, name="h1_s", align_bytes=64)
-            quantise(h1_grouped[r], h1_c, h1_s)
-            h1_codes[r] = h1_c
-            h1_scales[r] = h1_s
 
         def layer_two(r, i, engines):
             if i == 0:
@@ -240,8 +233,8 @@ def tile_mybadtransfomerblock_pa_kernel(tc, x, pos_emb, enc_w0, enc_w1, out):
                 for g in range(PASSES):
                     nc.tensor.matmul_mx(
                         out=bank[:],
-                        lhsT=h1_codes[r][:, g, i * P : (i + 1) * P].bitcast(FP8X4),
-                        lhsT_scale=h1_scales[r][:, g, i * P : (i + 1) * P],
+                        lhsT=codes["h1", r][:, g, i * P : (i + 1) * P].bitcast(FP8X4),
+                        lhsT_scale=scales["h1", r][:, g, i * P : (i + 1) * P],
                         rhs=codes_of["w1", n][:, g, :].bitcast(FP8X4),
                         rhs_scale=scales_of["w1", n][:, g, :],
                         start=(g == 0),
@@ -253,7 +246,7 @@ def tile_mybadtransfomerblock_pa_kernel(tc, x, pos_emb, enc_w0, enc_w1, out):
                 else:
                     nc.scalar.activation(out=h2_half, in_=bank[:], func=ACT.Relu)
 
-        def take_norms(tiles):
+        def sum_squares(tiles):
             sum_sq = four.tile([P, PAIR], F32, name="sum_sq")
             for c, (r, i) in enumerate(tiles):
                 squares = two.tile([P, D], BF16, name="squares")
@@ -263,15 +256,20 @@ def tile_mybadtransfomerblock_pa_kernel(tc, x, pos_emb, enc_w0, enc_w1, out):
                     func=ACT.Square,
                     accum_out=sum_sq[:, c : c + 1],
                 )
-            norm_t = four.tile([P, PAIR], F32, name="norm_t")
-            nc.scalar.sqrt(norm_t[:, : len(tiles)], sum_sq[:, : len(tiles)])
-            norm[tiles] = norm_t
+            sums[tiles] = sum_sq
+
+        def take_roots(tiles):
+            norm = four.tile([P, PAIR], F32, name="norm")
+            nc.scalar.sqrt(norm[:, : len(tiles)], sums[tiles][:, : len(tiles)])
+            norms[tiles] = norm
+
+        def add_eps(tiles):
+            some = norms[tiles][:, : len(tiles)]
+            nc.vector.tensor_scalar_add(out=some, in0=some, scalar1=EPS)
 
         def invert_norms(tiles):
             inverse = four.tile([P, PAIR], F32, name="inverse")
-            some = inverse[:, : len(tiles)]
-            nc.vector.tensor_scalar_add(out=some, in0=norm[tiles][:, : len(tiles)], scalar1=EPS)
-            nc.vector.reciprocal(out=some, in_=some)
+            nc.vector.reciprocal(out=inverse[:, : len(tiles)], in_=norms[tiles][:, : len(tiles)])
             inverses[tiles] = inverse
 
         def scale(tiles, engine):
@@ -284,43 +282,42 @@ def tile_mybadtransfomerblock_pa_kernel(tc, x, pos_emb, enc_w0, enc_w1, out):
                     op0=ALU.mult,
                     op1=ALU.add,
                 )
-                nc.sync.dma_start(out=out_rounds[r][:, i, :], in_=h2[r][:, i, :])
+                nc.sync.dma_start(out=out_rounds[token_round(r)][:, i, :], in_=h2[r][:, i, :])
 
-        inverses = {}
         scalar_copy = nc.scalar.copy
         vector_copy = nc.vector.tensor_copy
         both = (scalar_copy, vector_copy)
         scalar_only = (scalar_copy, scalar_copy)
-        y_engines = both
         on_vector = ("vector", "vector")
+
+        on_vector_twice = (nc.vector, nc.vector)
 
         halve_w0(0, 0)
         transpose_w0(0, 0, scalar_only)
-        add_positions(0)
+        add_positions(0, on_vector_twice)
         quantise_w0(0, 0)
-        transpose_y(0)
+        transpose_y(0, both)
         halve_w0(0, 1)
         transpose_w0(0, 1, scalar_only)
         halve_w0(1, 0)
         transpose_w0(1, 0, scalar_only)
-        quantise_y(0)
+        quantise_round("y", 0)
         halve_w0(1, 1)
         quantise_w0(0, 1)
         transpose_w0(1, 1, scalar_only)
         quantise_w0(1, 0)
         layer_one(0, 0)
         quantise_w0(1, 1)
-        add_positions(1)
+        add_positions(1, on_vector_twice)
         transpose_w1(0, 0, scalar_only)
-        transpose_w1(0, 1, scalar_only)
+        transpose_w1(0, 1, both)
         layer_one(0, 1)
         quantise_w1(0)
-        transpose_y(1)
-        add_positions(2)
-        quantise_y(1)
+        transpose_y(1, both)
+        add_positions(2, on_vector_twice)
+        quantise_round("y", 1)
         transpose_w1(1, 0, scalar_only)
         transpose_w1(1, 1, scalar_only)
-        quantise_h1(0)
         quantise_w1(1)
 
         groups = {0: ((0, 0),), ROUNDS: ((ROUNDS - 1, 1),)}
@@ -329,25 +326,33 @@ def tile_mybadtransfomerblock_pa_kernel(tc, x, pos_emb, enc_w0, enc_w1, out):
 
         for s in range(2, ROUNDS + 2):
             k = s - 2
+            if s < ROUNDS + 1:
+                quantise_round("h1", k)
+            if 1 <= k:
+                take_roots(groups[k - 1])
             if s < ROUNDS:
-                transpose_y(s)
+                transpose_y(s, both if s % 2 else scalar_only)
+            if s + 1 < ROUNDS:
+                add_positions(s + 1, on_vector_twice)
+            if 1 <= k:
+                add_eps(groups[k - 1])
+            if s < ROUNDS:
+                quantise_round("y", s)
             if s - 1 < ROUNDS:
                 layer_one(s - 1, 0)
                 layer_one(s - 1, 1)
-            if s + 1 < ROUNDS:
-                add_positions(s + 1)
-            if s < ROUNDS:
-                quantise_y(s)
             if 1 <= k:
                 invert_norms(groups[k - 1])
                 scale(groups[k - 1], nc.gpsimd)
             layer_two(k, 0, on_vector)
-            if s - 1 < ROUNDS:
-                quantise_h1(s - 1)
-            take_norms(groups[k])
+            if s == ROUNDS:
+                quantise_round("h1", k + 1)
+            sum_squares(groups[k])
             layer_two(k, 1, on_vector)
-        invert_norms(groups[ROUNDS - 1])
-        scale(groups[ROUNDS - 1], nc.vector)
-        take_norms(groups[ROUNDS])
-        invert_norms(groups[ROUNDS])
-        scale(groups[ROUNDS], nc.vector)
+        for tiles in (groups[ROUNDS - 1], groups[ROUNDS]):
+            if tiles == groups[ROUNDS]:
+                sum_squares(tiles)
+            take_roots(tiles)
+            add_eps(tiles)
+            invert_norms(tiles)
+            scale(tiles, nc.vector)

@@ -26,7 +26,6 @@ BATCH = ROUNDS // POS_ROUNDS
 HALF = 512
 HALVES = D // HALF
 HALF_BLOCK = 16
-BLOCKS = K_PASS // (2 * HALF_BLOCK)
 EPS = 1e-6
 
 FLOPS = 2 * 2 * TOKENS * D * D
@@ -63,6 +62,13 @@ def tile_mybadtransfomerblock_pa_kernel(tc, x, pos_emb, enc_w0, enc_w1, out):
             nc.sync.dma_start(out=rows[:], in_=source)
             return rows
 
+        def load_by_rows(first, second):
+            pair = [raw.tile([P, PAIR, D], BF16, name="%s_sb0" % name) for name in ("x", "pos")]
+            for i in range(PAIR):
+                for rows, source in zip(pair, (first, second)):
+                    nc.sync.dma_start(out=rows[:, i, :], in_=source[:, i, :])
+            return pair
+
         def token_round(r):
             return r % BATCH * POS_ROUNDS + r // BATCH
 
@@ -71,8 +77,7 @@ def tile_mybadtransfomerblock_pa_kernel(tc, x, pos_emb, enc_w0, enc_w1, out):
         w0_sb = {}
         w1_sb = {}
         w0_sb[0, 0] = load("w0_sb00", w0_halves[0][:, 0:2, :])
-        x_sb[0] = load("x_sb0", x_rounds[token_round(0)])
-        pos_sb[0] = load("pos_sb0", pos_rounds[0])
+        x_sb[0], pos_sb[0] = load_by_rows(x_rounds[token_round(0)], pos_rounds[0])
         w0_sb[0, 1] = load("w0_sb01", w0_halves[0][:, 2:4, :])
         w0_sb[1, 0] = load("w0_sb10", w0_halves[1][:, 0:2, :])
         w0_sb[1, 1] = load("w0_sb11", w0_halves[1][:, 2:4, :])
@@ -98,34 +103,36 @@ def tile_mybadtransfomerblock_pa_kernel(tc, x, pos_emb, enc_w0, enc_w1, out):
 
         grouped_of = {}
 
-        def blocks(rows):
-            return rows[:].rearrange("p i (g b u n) -> p (i g) u b n", u=2, b=BLOCKS, n=HALF_BLOCK)
-
-        def halved(rows):
-            return rows[:].rearrange("p i (g u b n) -> p (i g) u b n", u=2, b=BLOCKS, n=HALF_BLOCK)
+        def by_halves(rows):
+            return rows[:].rearrange("p i (c u n) -> p u (i c) n", u=2, n=HALF_BLOCK)
 
         w0_rows = {}
 
         def halve_w0(h, c):
-            w_rows = three.tile([P, PAIR, D], BF16, name="w_rows")
-            for u in range(2):
-                nc.vector.tensor_copy(out=halved(w_rows)[:, :, u], in_=blocks(w0_sb[h, c])[:, :, u])
+            w_rows = three.tile([P, 2, PAIR * D // 2], BF16, name="w_rows")
+            nc.vector.tensor_copy(
+                out=w_rows[:].rearrange("p u (c n) -> p u c n", n=HALF_BLOCK),
+                in_=by_halves(w0_sb[h, c]),
+            )
             w0_rows[h, c] = w_rows
 
-        def transpose_halved(words, grouped, i, copy_out):
-            bank = psum.tile([P, 2 * PASSES, P], F32, tag="bank")
-            for c in range(2 * PASSES):
-                nc.tensor.transpose(bank[:, c, :], words[:, c * P : (c + 1) * P], ident[:])
+        def transpose_halved(rows, grouped, i, copy_out):
+            words = rows[:].bitcast(F32)
+            bank = psum.tile([P, PASSES, 2, P], F32, tag="bank")
+            for g in range(PASSES):
+                for u in range(2):
+                    first = (PASSES * i + g) * P
+                    nc.tensor.transpose(bank[:, g, u, :], words[:, u, first : first + P], ident[:])
             copy_out(
                 out=grouped.bitcast(F32)[:, :, i * P : (i + 1) * P, :],
-                in_=bank[:].rearrange("p (g u) c -> p g c u", u=2),
+                in_=bank[:].rearrange("p g u c -> p g c u"),
             )
 
         def transpose_w0(h, c, engines):
             w0_grouped = three.tile([P, PASSES, ROUND, PACK], BF16, name="w0_grouped", align_bytes=64)
             grouped_of["w0", h, c] = w0_grouped
             for e in range(PAIR):
-                transpose_halved(w0_rows[h, c][:, e, :].bitcast(F32), w0_grouped[:], e, engines[e])
+                transpose_halved(w0_rows[h, c], w0_grouped[:], e, engines[e])
 
         def quantise_w0(h, c):
             w_codes = keep.tile([P, PASSES, ROUND], U32, name="w0_codes%d%d" % (h, c), align_bytes=64)
@@ -183,13 +190,19 @@ def tile_mybadtransfomerblock_pa_kernel(tc, x, pos_emb, enc_w0, enc_w1, out):
             codes[kind, r] = packed
             scales[kind, r] = bytes_of
 
-        def add_positions(r, engines):
-            y = three.tile([P, PAIR, D], BF16, name="y_rows")
-            for u in range(2):
-                engines[u].tensor_tensor(
-                    out=halved(y)[:, :, u],
-                    in0=blocks(x_sb[r])[:, :, u],
-                    in1=blocks(pos_sb[r // BATCH])[:, :, u],
+        def add_positions(r):
+            y = three.tile([P, 2, PAIR * D // 2], BF16, name="y_rows")
+            y_halves = y[:].rearrange("p u (c n) -> p u c n", n=HALF_BLOCK)
+            x_halves = by_halves(x_sb[r])
+            pos_halves = by_halves(pos_sb[r // BATCH])
+            blocks = PAIR * D // (2 * HALF_BLOCK)
+            step = blocks // PAIR if r == 0 else blocks
+            for first in range(0, blocks, step):
+                some = slice(first, first + step)
+                nc.vector.tensor_tensor(
+                    out=y_halves[:, :, some],
+                    in0=x_halves[:, :, some],
+                    in1=pos_halves[:, :, some],
                     op=ALU.add,
                 )
             y_rows[r] = y
@@ -197,9 +210,9 @@ def tile_mybadtransfomerblock_pa_kernel(tc, x, pos_emb, enc_w0, enc_w1, out):
         def transpose_y(r, engines):
             new_grouped("y", r)
             for i in range(PAIR):
-                transpose_halved(y_rows[r][:, i, :].bitcast(F32), grouped["y", r][:], i, engines[i])
+                transpose_halved(y_rows[r], grouped["y", r][:], i, engines[i])
 
-        def layer_one(r, q):
+        def layer_one(r, q, on_vector=False):
             if q == 0:
                 new_grouped("h1", r)
             for i in range(PAIR):
@@ -218,11 +231,12 @@ def tile_mybadtransfomerblock_pa_kernel(tc, x, pos_emb, enc_w0, enc_w1, out):
                             start=(g == 0),
                             stop=(g == PASSES - 1),
                         )
-                nc.scalar.activation(
-                    out=grouped["h1", r][:, q, i * P : (i + 1) * P, :],
-                    in_=bank[:].rearrange("p t c -> p c t"),
-                    func=ACT.Relu,
-                )
+                h1 = grouped["h1", r][:, q, i * P : (i + 1) * P, :]
+                products = bank[:].rearrange("p t c -> p c t")
+                if on_vector:
+                    nc.vector.tensor_scalar_max(out=h1, in0=products, scalar1=0.0)
+                else:
+                    nc.scalar.activation(out=h1, in_=products, func=ACT.Relu)
 
         def layer_two(r, i, engines):
             if i == 0:
@@ -246,35 +260,38 @@ def tile_mybadtransfomerblock_pa_kernel(tc, x, pos_emb, enc_w0, enc_w1, out):
                 else:
                     nc.scalar.activation(out=h2_half, in_=bank[:], func=ACT.Relu)
 
-        def sum_squares(tiles):
-            sum_sq = four.tile([P, PAIR], F32, name="sum_sq")
-            for c, (r, i) in enumerate(tiles):
-                squares = two.tile([P, D], BF16, name="squares")
-                nc.scalar.activation(
-                    out=squares[:],
-                    in_=h2[r][:, i, :],
-                    func=ACT.Square,
-                    accum_out=sum_sq[:, c : c + 1],
-                )
-            sums[tiles] = sum_sq
+        def square(tiles, c):
+            if c == 0:
+                sum_sq = four.tile([P, PAIR], F32, name="sum_sq")
+                sums[tiles] = sum_sq
+            r, i = tiles[c]
+            squares = two.tile([P, D], BF16, name="squares")
+            nc.scalar.activation(
+                out=squares[:],
+                in_=h2[r][:, i, :],
+                func=ACT.Square,
+                accum_out=sums[tiles][:, c : c + 1],
+            )
 
         def take_roots(tiles):
             norm = four.tile([P, PAIR], F32, name="norm")
             nc.scalar.sqrt(norm[:, : len(tiles)], sums[tiles][:, : len(tiles)])
             norms[tiles] = norm
 
-        def add_eps(tiles):
+        def add_eps(tiles, eps_engine):
             some = norms[tiles][:, : len(tiles)]
-            nc.vector.tensor_scalar_add(out=some, in0=some, scalar1=EPS)
+            eps_engine.tensor_scalar(
+                out=some, in0=some, scalar1=EPS, scalar2=0.0, op0=ALU.add, op1=ALU.add
+            )
 
         def invert_norms(tiles):
             inverse = four.tile([P, PAIR], F32, name="inverse")
             nc.vector.reciprocal(out=inverse[:, : len(tiles)], in_=norms[tiles][:, : len(tiles)])
             inverses[tiles] = inverse
 
-        def scale(tiles, engine):
+        def scale(tiles, *engines):
             for c, (r, i) in enumerate(tiles):
-                engine.tensor_scalar(
+                engines[c % len(engines)].tensor_scalar(
                     out=h2[r][:, i, :],
                     in0=h2[r][:, i, :],
                     scalar1=inverses[tiles][:, c : c + 1],
@@ -290,11 +307,17 @@ def tile_mybadtransfomerblock_pa_kernel(tc, x, pos_emb, enc_w0, enc_w1, out):
         scalar_only = (scalar_copy, scalar_copy)
         on_vector = ("vector", "vector")
 
-        on_vector_twice = (nc.vector, nc.vector)
+        def scale_halves(tiles):
+            ((r, i),) = tiles
+            for n in range(HALVES):
+                features = slice(n * HALF, (n + 1) * HALF)
+                half = h2[r][:, i, features]
+                nc.vector.tensor_scalar_mul(out=half, in0=half, scalar1=inverses[tiles][:, 0:1])
+                nc.sync.dma_start(out=out_rounds[token_round(r)][:, i, features], in_=half)
 
         halve_w0(0, 0)
         transpose_w0(0, 0, scalar_only)
-        add_positions(0, on_vector_twice)
+        add_positions(0)
         quantise_w0(0, 0)
         transpose_y(0, both)
         halve_w0(0, 1)
@@ -308,13 +331,13 @@ def tile_mybadtransfomerblock_pa_kernel(tc, x, pos_emb, enc_w0, enc_w1, out):
         quantise_w0(1, 0)
         layer_one(0, 0)
         quantise_w0(1, 1)
-        add_positions(1, on_vector_twice)
+        add_positions(1)
         transpose_w1(0, 0, scalar_only)
         transpose_w1(0, 1, both)
         layer_one(0, 1)
         quantise_w1(0)
         transpose_y(1, both)
-        add_positions(2, on_vector_twice)
+        add_positions(2)
         quantise_round("y", 1)
         transpose_w1(1, 0, scalar_only)
         transpose_w1(1, 1, scalar_only)
@@ -324,35 +347,55 @@ def tile_mybadtransfomerblock_pa_kernel(tc, x, pos_emb, enc_w0, enc_w1, out):
         for k in range(1, ROUNDS):
             groups[k] = ((k - 1, 1), (k, 0))
 
-        for s in range(2, ROUNDS + 2):
+        for s in range(2, ROUNDS):
             k = s - 2
-            if s < ROUNDS + 1:
-                quantise_round("h1", k)
+            quantise_round("h1", k)
             if 1 <= k:
                 take_roots(groups[k - 1])
-            if s < ROUNDS:
-                transpose_y(s, both if s % 2 else scalar_only)
+            transpose_y(s, both if s % 2 else scalar_only)
             if s + 1 < ROUNDS:
-                add_positions(s + 1, on_vector_twice)
+                add_positions(s + 1)
             if 1 <= k:
-                add_eps(groups[k - 1])
-            if s < ROUNDS:
-                quantise_round("y", s)
-            if s - 1 < ROUNDS:
-                layer_one(s - 1, 0)
-                layer_one(s - 1, 1)
+                add_eps(groups[k - 1], nc.vector)
+            quantise_round("y", s)
+            layer_one(s - 1, 0)
+            layer_one(s - 1, 1)
             if 1 <= k:
                 invert_norms(groups[k - 1])
                 scale(groups[k - 1], nc.gpsimd)
             layer_two(k, 0, on_vector)
-            if s == ROUNDS:
-                quantise_round("h1", k + 1)
-            sum_squares(groups[k])
+            for c in range(len(groups[k])):
+                square(groups[k], c)
             layer_two(k, 1, on_vector)
-        for tiles in (groups[ROUNDS - 1], groups[ROUNDS]):
-            if tiles == groups[ROUNDS]:
-                sum_squares(tiles)
-            take_roots(tiles)
-            add_eps(tiles)
-            invert_norms(tiles)
-            scale(tiles, nc.vector)
+
+        last = ROUNDS - 1
+        shared = ("vector", "scalar")
+        quantise_round("h1", last - 1)
+        take_roots(groups[last - 2])
+        layer_one(last, 0)
+        layer_one(last, 1, on_vector=True)
+        square(groups[last - 1], 0)
+        quantise_round("h1", last)
+        add_eps(groups[last - 2], nc.vector)
+        layer_two(last - 1, 0, shared)
+        invert_norms(groups[last - 2])
+        scale(groups[last - 2], nc.gpsimd)
+        square(groups[last - 1], 1)
+        layer_two(last - 1, 1, on_vector)
+        take_roots(groups[last - 1])
+        square(groups[last], 0)
+        add_eps(groups[last - 1], nc.vector)
+        layer_two(last, 0, shared)
+        invert_norms(groups[last - 1])
+        scale(groups[last - 1], nc.gpsimd)
+        square(groups[last], 1)
+        layer_two(last, 1, on_vector)
+        take_roots(groups[last])
+        square(groups[ROUNDS], 0)
+        add_eps(groups[last], nc.vector)
+        invert_norms(groups[last])
+        scale(groups[last], nc.vector)
+        take_roots(groups[ROUNDS])
+        add_eps(groups[ROUNDS], nc.vector)
+        invert_norms(groups[ROUNDS])
+        scale_halves(groups[ROUNDS])

@@ -278,11 +278,9 @@ def tile_mybadtransfomerblock_pa_kernel(tc, x, pos_emb, enc_w0, enc_w1, out):
             nc.scalar.sqrt(norm[:, : len(tiles)], sums[tiles][:, : len(tiles)])
             norms[tiles] = norm
 
-        def add_eps(tiles, eps_engine):
+        def add_eps(tiles):
             some = norms[tiles][:, : len(tiles)]
-            eps_engine.tensor_scalar(
-                out=some, in0=some, scalar1=EPS, scalar2=0.0, op0=ALU.add, op1=ALU.add
-            )
+            nc.vector.tensor_scalar_add(out=some, in0=some, scalar1=EPS)
 
         def invert_norms(tiles):
             inverse = four.tile([P, PAIR], F32, name="inverse")
@@ -307,6 +305,14 @@ def tile_mybadtransfomerblock_pa_kernel(tc, x, pos_emb, enc_w0, enc_w1, out):
         scalar_only = (scalar_copy, scalar_copy)
         on_vector = ("vector", "vector")
 
+        zeros = const.tile([P, HALF], BF16)
+        nc.vector.memset(zeros[:], 0.0)
+
+        def keep_warm(count):
+            bank = psum.tile([P, HALF], F32, tag="bank")
+            for c in range(count):
+                nc.tensor.matmul(bank[:], lhsT=zeros[:, :P], rhs=zeros[:], start=True, stop=True)
+
         def scale_halves(tiles):
             ((r, i),) = tiles
             for n in range(HALVES):
@@ -315,17 +321,21 @@ def tile_mybadtransfomerblock_pa_kernel(tc, x, pos_emb, enc_w0, enc_w1, out):
                 nc.vector.tensor_scalar_mul(out=half, in0=half, scalar1=inverses[tiles][:, 0:1])
                 nc.sync.dma_start(out=out_rounds[token_round(r)][:, i, features], in_=half)
 
+        keep_warm(7)
         halve_w0(0, 0)
         transpose_w0(0, 0, scalar_only)
+        keep_warm(3)
         add_positions(0)
         quantise_w0(0, 0)
         transpose_y(0, both)
+        keep_warm(3)
         halve_w0(0, 1)
         transpose_w0(0, 1, scalar_only)
         halve_w0(1, 0)
         transpose_w0(1, 0, scalar_only)
         quantise_round("y", 0)
         halve_w0(1, 1)
+        keep_warm(2)
         quantise_w0(0, 1)
         transpose_w0(1, 1, scalar_only)
         quantise_w0(1, 0)
@@ -333,6 +343,7 @@ def tile_mybadtransfomerblock_pa_kernel(tc, x, pos_emb, enc_w0, enc_w1, out):
         quantise_w0(1, 1)
         add_positions(1)
         transpose_w1(0, 0, scalar_only)
+        keep_warm(2)
         transpose_w1(0, 1, both)
         layer_one(0, 1)
         quantise_w1(0)
@@ -340,6 +351,7 @@ def tile_mybadtransfomerblock_pa_kernel(tc, x, pos_emb, enc_w0, enc_w1, out):
         add_positions(2)
         quantise_round("y", 1)
         transpose_w1(1, 0, scalar_only)
+        keep_warm(2)
         transpose_w1(1, 1, scalar_only)
         quantise_w1(1)
 
@@ -356,7 +368,7 @@ def tile_mybadtransfomerblock_pa_kernel(tc, x, pos_emb, enc_w0, enc_w1, out):
             if s + 1 < ROUNDS:
                 add_positions(s + 1)
             if 1 <= k:
-                add_eps(groups[k - 1], nc.vector)
+                add_eps(groups[k - 1])
             quantise_round("y", s)
             layer_one(s - 1, 0)
             layer_one(s - 1, 1)
@@ -376,26 +388,31 @@ def tile_mybadtransfomerblock_pa_kernel(tc, x, pos_emb, enc_w0, enc_w1, out):
         layer_one(last, 1, on_vector=True)
         square(groups[last - 1], 0)
         quantise_round("h1", last)
-        add_eps(groups[last - 2], nc.vector)
+        add_eps(groups[last - 2])
         layer_two(last - 1, 0, shared)
         invert_norms(groups[last - 2])
         scale(groups[last - 2], nc.gpsimd)
         square(groups[last - 1], 1)
         layer_two(last - 1, 1, on_vector)
         take_roots(groups[last - 1])
-        square(groups[last], 0)
-        add_eps(groups[last - 1], nc.vector)
+        tile_a, tile_b = ((last - 1, 1),), ((last, 0),)
+        square(tile_a, 0)
+        add_eps(groups[last - 1])
+        take_roots(tile_a)
         layer_two(last, 0, shared)
         invert_norms(groups[last - 1])
-        scale(groups[last - 1], nc.gpsimd)
-        square(groups[last], 1)
+        scale(groups[last - 1], nc.gpsimd, nc.vector)
+        square(tile_b, 0)
+        add_eps(tile_a)
         layer_two(last, 1, on_vector)
-        take_roots(groups[last])
+        invert_norms(tile_a)
+        scale(tile_a, nc.vector)
+        take_roots(tile_b)
         square(groups[ROUNDS], 0)
-        add_eps(groups[last], nc.vector)
-        invert_norms(groups[last])
-        scale(groups[last], nc.vector)
+        add_eps(tile_b)
+        invert_norms(tile_b)
+        scale(tile_b, nc.vector)
         take_roots(groups[ROUNDS])
-        add_eps(groups[ROUNDS], nc.vector)
+        add_eps(groups[ROUNDS])
         invert_norms(groups[ROUNDS])
         scale_halves(groups[ROUNDS])

@@ -364,7 +364,7 @@ def tile_mybadtransfomerblock_pa_kernel(tc, x, pos_emb, enc_w0, enc_w1, out):
             quantise_round("h1", k)
             if 1 <= k:
                 take_roots(groups[k - 1])
-            transpose_y(s, both if s % 2 else scalar_only)
+            transpose_y(s, scalar_only if s < 4 else both)
             if s + 1 < ROUNDS:
                 add_positions(s + 1)
             if 1 <= k:

from contextlib import ExitStack

import concourse.mybir as mybir
from concourse.masks import make_identity

BF16 = mybir.dt.bfloat16
F32 = mybir.dt.float32
U32 = mybir.dt.uint32
U8 = mybir.dt.uint8
FP8X4 = mybir.dt.float8_e4m3fn_x4
ACT = mybir.ActivationFunctionType
ALU = mybir.AluOpType

P = 128
D = 1024
TOKENS = 2048
POSITIONS = 1024
PACK = 4
K_PASS = P * PACK
PASSES = D // K_PASS
PAIR = 2
ROUND = PAIR * P
ROUNDS = TOKENS // ROUND
POS_ROUNDS = POSITIONS // ROUND
BATCH = ROUNDS // POS_ROUNDS
HALF = 512
HALVES = D // HALF
HALF_BLOCK = 16
EPS = 1e-6

FLOPS = 2 * 2 * TOKENS * D * D


def tile_mybadtransfomerblock_pa_kernel(tc, x, pos_emb, enc_w0, enc_w1, out):
    nc = tc.nc

    x_rounds = x.flatten_outer_dims().rearrange("(r p i) d -> r p i d", p=P, i=PAIR)
    pos_rounds = pos_emb.flatten_outer_dims().rearrange("(r p i) d -> r p i d", p=P, i=PAIR)
    out_rounds = out.flatten_outer_dims().rearrange("(r p i) d -> r p i d", p=P, i=PAIR)
    w0_halves = enc_w0.rearrange("(h p j) k -> h p j k", p=P, j=PACK)
    w1_halves = enc_w1.rearrange("(h j p) k -> h p j k", p=P, j=PACK)

    with ExitStack() as ctx:
        const = ctx.enter_context(tc.tile_pool(name="const", bufs=1))
        raw = ctx.enter_context(tc.tile_pool(name="raw", bufs=1))
        keep = ctx.enter_context(tc.tile_pool(name="keep", bufs=1))
        two = ctx.enter_context(tc.tile_pool(name="two", bufs=2))
        three = ctx.enter_context(tc.tile_pool(name="three", bufs=3))
        four = ctx.enter_context(tc.tile_pool(name="four", bufs=4))
        psum = ctx.enter_context(tc.psum_pool(name="psum", bufs=8))
        ctx.enter_context(tc.manual_schedule())

        warm = const.tile([P, 1], F32)
        nc.vector.memset(warm[:], 1.0)
        nc.scalar.sqrt(warm[:], warm[:])

        ident = const.tile([P, P], F32)
        make_identity(nc, ident[:])

        def load(name, source):
            rows = raw.tile([P, PAIR, D], BF16, name=name)
            nc.sync.dma_start(out=rows[:], in_=source)
            return rows

        def load_by_rows(first, second):
            pair = [raw.tile([P, PAIR, D], BF16, name="%s_sb0" % name) for name in ("x", "pos")]
            for i in range(PAIR):
                for rows, source in zip(pair, (first, second)):
                    nc.sync.dma_start(out=rows[:, i, :], in_=source[:, i, :])
            return pair

        def token_round(r):
            return r % BATCH * POS_ROUNDS + r // BATCH

        x_sb = {}
        pos_sb = {}
        w0_sb = {}
        w1_sb = {}
        w0_sb[0, 0] = load("w0_sb00", w0_halves[0][:, 0:2, :])
        x_sb[0], pos_sb[0] = load_by_rows(x_rounds[token_round(0)], pos_rounds[0])
        w0_sb[0, 1] = load("w0_sb01", w0_halves[0][:, 2:4, :])
        w0_sb[1, 0] = load("w0_sb10", w0_halves[1][:, 0:2, :])
        w0_sb[1, 1] = load("w0_sb11", w0_halves[1][:, 2:4, :])
        w1_sb[0, 0] = load("w1_sb00", w1_halves[0][:, 0:2, :])
        w1_sb[0, 1] = load("w1_sb01", w1_halves[0][:, 2:4, :])
        x_sb[1] = load("x_sb1", x_rounds[token_round(1)])
        w1_sb[1, 0] = load("w1_sb10", w1_halves[1][:, 0:2, :])
        w1_sb[1, 1] = load("w1_sb11", w1_halves[1][:, 2:4, :])
        for r in range(2, ROUNDS):
            if r % BATCH == 0:
                pos_sb[r // BATCH] = load("pos_sb%d" % (r // BATCH), pos_rounds[r // BATCH])
            x_sb[r] = load("x_sb%d" % r, x_rounds[token_round(r)])

        def quantise(grouped, codes, scales):
            nc.vector.quantize_mx(
                out=codes[:].rearrange("p g c -> p (g c)").bitcast(FP8X4),
                scales=scales[:].rearrange("p g c -> p (g c)"),
                in_=grouped[:].rearrange("p g c t -> p (g c t)"),
            )

        codes_of = {}
        scales_of = {}

        grouped_of = {}

        def by_halves(rows):
            return rows[:].rearrange("p i (c u n) -> p u (i c) n", u=2, n=HALF_BLOCK)

        w0_rows = {}

        def halve_w0(h, c):
            w_rows = three.tile([P, 2, PAIR * D // 2], BF16, name="w_rows")
            nc.vector.tensor_copy(
                out=w_rows[:].rearrange("p u (c n) -> p u c n", n=HALF_BLOCK),
                in_=by_halves(w0_sb[h, c]),
            )
            w0_rows[h, c] = w_rows

        def transpose_halved(rows, grouped, i, copy_out):
            words = rows[:].bitcast(F32)
            bank = psum.tile([P, PASSES, 2, P], F32, tag="bank")
            for g in range(PASSES):
                for u in range(2):
                    first = (PASSES * i + g) * P
                    nc.tensor.transpose(bank[:, g, u, :], words[:, u, first : first + P], ident[:])
            copy_out(
                out=grouped.bitcast(F32)[:, :, i * P : (i + 1) * P, :],
                in_=bank[:].rearrange("p g u c -> p g c u"),
            )

        def transpose_w0(h, c, engines):
            w0_grouped = three.tile([P, PASSES, ROUND, PACK], BF16, name="w0_grouped", align_bytes=64)
            grouped_of["w0", h, c] = w0_grouped
            for e in range(PAIR):
                transpose_halved(w0_rows[h, c], w0_grouped[:], e, engines[e])

        def quantise_w0(h, c):
            w_codes = keep.tile([P, PASSES, ROUND], U32, name="w0_codes%d%d" % (h, c), align_bytes=64)
            w_scales = keep.tile([P, PASSES, ROUND], U8, name="w0_scales%d%d" % (h, c), align_bytes=64)
            quantise(grouped_of["w0", h, c], w_codes, w_scales)
            codes_of["w0", h, c] = w_codes
            scales_of["w0", h, c] = w_scales

        def transpose_w1(h, c, engines):
            if c == 0:
                w1_grouped = two.tile([P, PASSES, HALF, PACK], BF16, name="w1_grouped", align_bytes=64)
                grouped_of["w1", h] = w1_grouped
            for e in range(PAIR):
                j = PAIR * c + e
                words = w1_sb[h, c][:, e, :].bitcast(F32)
                bank = psum.tile([P, 2 * PASSES, P], F32, tag="bank")
                for g in range(PASSES):
                    for u in range(2):
                        nc.tensor.transpose(
                            bank[:, 2 * g + u, :],
                            words[:, 2 * P * g + u : 2 * P * (g + 1) : 2],
                            ident[:],
                        )
                engines[e](
                    out=grouped_of["w1", h][:].bitcast(F32)[:, :, j * P : (j + 1) * P, :],
                    in_=bank[:].rearrange("p (g u) c -> p g c u", u=2),
                )

        def quantise_w1(h):
            w_codes = keep.tile([P, PASSES, HALF], U32, name="w1_codes%d" % h, align_bytes=64)
            w_scales = keep.tile([P, PASSES, HALF], U8, name="w1_scales%d" % h, align_bytes=64)
            quantise(grouped_of["w1", h], w_codes, w_scales)
            codes_of["w1", h] = w_codes
            scales_of["w1", h] = w_scales

        y_rows = {}
        grouped = {}
        codes = {}
        scales = {}
        h2 = {}
        sums = {}
        norms = {}
        inverses = {}

        def new_grouped(kind, r):
            values = three.tile(
                [P, PASSES, ROUND, PACK], BF16, name="%s_grouped" % kind, align_bytes=64
            )
            grouped[kind, r] = values

        def quantise_round(kind, r):
            packed = three.tile([P, PASSES, ROUND], U32, name="%s_codes" % kind, align_bytes=64)
            bytes_of = three.tile([P, PASSES, ROUND], U8, name="%s_scales" % kind, align_bytes=64)
            quantise(grouped[kind, r], packed, bytes_of)
            codes[kind, r] = packed
            scales[kind, r] = bytes_of

        def add_positions(r):
            y = three.tile([P, 2, PAIR * D // 2], BF16, name="y_rows")
            y_halves = y[:].rearrange("p u (c n) -> p u c n", n=HALF_BLOCK)
            x_halves = by_halves(x_sb[r])
            pos_halves = by_halves(pos_sb[r // BATCH])
            blocks = PAIR * D // (2 * HALF_BLOCK)
            step = blocks // PAIR if r == 0 else blocks
            for first in range(0, blocks, step):
                some = slice(first, first + step)
                nc.vector.tensor_tensor(
                    out=y_halves[:, :, some],
                    in0=x_halves[:, :, some],
                    in1=pos_halves[:, :, some],
                    op=ALU.add,
                )
            y_rows[r] = y

        def transpose_y(r, engines):
            new_grouped("y", r)
            for i in range(PAIR):
                transpose_halved(y_rows[r], grouped["y", r][:], i, engines[i])

        def layer_one(r, q, on_vector=False):
            if q == 0:
                new_grouped("h1", r)
            for i in range(PAIR):
                bank = psum.tile([P, PACK, P], F32, tag="bank")
                for t in range(PACK):
                    w_codes = codes_of["w0", q, t // PAIR]
                    w_scales = scales_of["w0", q, t // PAIR]
                    features = slice(t % PAIR * P, (t % PAIR + 1) * P)
                    for g in range(PASSES):
                        nc.tensor.matmul_mx(
                            out=bank[:, t, :],
                            lhsT=w_codes[:, g, features].bitcast(FP8X4),
                            lhsT_scale=w_scales[:, g, features],
                            rhs=codes["y", r][:, g, i * P : (i + 1) * P].bitcast(FP8X4),
                            rhs_scale=scales["y", r][:, g, i * P : (i + 1) * P],
                            start=(g == 0),
                            stop=(g == PASSES - 1),
                        )
                h1 = grouped["h1", r][:, q, i * P : (i + 1) * P, :]
                products = bank[:].rearrange("p t c -> p c t")
                if on_vector:
                    nc.vector.tensor_scalar_max(out=h1, in0=products, scalar1=0.0)
                else:
                    nc.scalar.activation(out=h1, in_=products, func=ACT.Relu)

        def layer_two(r, i, engines):
            if i == 0:
                h2_r = four.tile([P, PAIR, D], F32, name="h2_r")
                h2[r] = h2_r
            for n in range(HALVES):
                bank = psum.tile([P, HALF], F32, tag="bank")
                for g in range(PASSES):
                    nc.tensor.matmul_mx(
                        out=bank[:],
                        lhsT=codes["h1", r][:, g, i * P : (i + 1) * P].bitcast(FP8X4),
                        lhsT_scale=scales["h1", r][:, g, i * P : (i + 1) * P],
                        rhs=codes_of["w1", n][:, g, :].bitcast(FP8X4),
                        rhs_scale=scales_of["w1", n][:, g, :],
                        start=(g == 0),
                        stop=(g == PASSES - 1),
                    )
                h2_half = h2[r][:, i, n * HALF : (n + 1) * HALF]
                if engines[n] == "vector":
                    nc.vector.tensor_scalar_max(out=h2_half, in0=bank[:], scalar1=0.0)
                else:
                    nc.scalar.activation(out=h2_half, in_=bank[:], func=ACT.Relu)

        def square(tiles, c):
            if c == 0:
                sum_sq = four.tile([P, PAIR], F32, name="sum_sq")
                sums[tiles] = sum_sq
            r, i = tiles[c]
            squares = two.tile([P, D], BF16, name="squares")
            nc.scalar.activation(
                out=squares[:],
                in_=h2[r][:, i, :],
                func=ACT.Square,
                accum_out=sums[tiles][:, c : c + 1],
            )

        def take_roots(tiles):
            norm = four.tile([P, PAIR], F32, name="norm")
            nc.scalar.sqrt(norm[:, : len(tiles)], sums[tiles][:, : len(tiles)])
            norms[tiles] = norm

        def add_eps(tiles):
            some = norms[tiles][:, : len(tiles)]
            nc.vector.tensor_scalar_add(out=some, in0=some, scalar1=EPS)

        def invert_norms(tiles):
            inverse = four.tile([P, PAIR], F32, name="inverse")
            nc.vector.reciprocal(out=inverse[:, : len(tiles)], in_=norms[tiles][:, : len(tiles)])
            inverses[tiles] = inverse

        def scale(tiles, *engines):
            for c, (r, i) in enumerate(tiles):
                engines[c % len(engines)].tensor_scalar(
                    out=h2[r][:, i, :],
                    in0=h2[r][:, i, :],
                    scalar1=inverses[tiles][:, c : c + 1],
                    scalar2=0.0,
                    op0=ALU.mult,
                    op1=ALU.add,
                )
                nc.sync.dma_start(out=out_rounds[token_round(r)][:, i, :], in_=h2[r][:, i, :])

        scalar_copy = nc.scalar.copy
        vector_copy = nc.vector.tensor_copy
        both = (scalar_copy, vector_copy)
        scalar_only = (scalar_copy, scalar_copy)
        on_vector = ("vector", "vector")

        zeros = const.tile([P, HALF], BF16)
        nc.vector.memset(zeros[:], 0.0)

        def keep_warm(count):
            bank = psum.tile([P, HALF], F32, tag="bank")
            for c in range(count):
                nc.tensor.matmul(bank[:], lhsT=zeros[:, :P], rhs=zeros[:], start=True, stop=True)

        def scale_halves(tiles):
            ((r, i),) = tiles
            for n in range(HALVES):
                features = slice(n * HALF, (n + 1) * HALF)
                half = h2[r][:, i, features]
                nc.vector.tensor_scalar_mul(out=half, in0=half, scalar1=inverses[tiles][:, 0:1])
                nc.sync.dma_start(out=out_rounds[token_round(r)][:, i, features], in_=half)

        keep_warm(7)
        halve_w0(0, 0)
        transpose_w0(0, 0, scalar_only)
        keep_warm(3)
        add_positions(0)
        quantise_w0(0, 0)
        transpose_y(0, both)
        keep_warm(3)
        halve_w0(0, 1)
        transpose_w0(0, 1, scalar_only)
        halve_w0(1, 0)
        transpose_w0(1, 0, scalar_only)
        quantise_round("y", 0)
        halve_w0(1, 1)
        keep_warm(2)
        quantise_w0(0, 1)
        transpose_w0(1, 1, scalar_only)
        quantise_w0(1, 0)
        layer_one(0, 0)
        quantise_w0(1, 1)
        add_positions(1)
        transpose_w1(0, 0, scalar_only)
        keep_warm(2)
        transpose_w1(0, 1, both)
        layer_one(0, 1)
        quantise_w1(0)
        transpose_y(1, both)
        add_positions(2)
        quantise_round("y", 1)
        transpose_w1(1, 0, scalar_only)
        keep_warm(2)
        transpose_w1(1, 1, scalar_only)
        quantise_w1(1)

        groups = {0: ((0, 0),), ROUNDS: ((ROUNDS - 1, 1),)}
        for k in range(1, ROUNDS):
            groups[k] = ((k - 1, 1), (k, 0))

        for s in range(2, ROUNDS):
            k = s - 2
            quantise_round("h1", k)
            if 1 <= k:
                take_roots(groups[k - 1])
            transpose_y(s, scalar_only if s < 4 else both)
            if s + 1 < ROUNDS:
                add_positions(s + 1)
            if 1 <= k:
                add_eps(groups[k - 1])
            quantise_round("y", s)
            layer_one(s - 1, 0)
            layer_one(s - 1, 1)
            if 1 <= k:
                invert_norms(groups[k - 1])
                scale(groups[k - 1], nc.gpsimd)
            layer_two(k, 0, on_vector)
            for c in range(len(groups[k])):
                square(groups[k], c)
            layer_two(k, 1, on_vector)

        last = ROUNDS - 1
        shared = ("vector", "scalar")
        quantise_round("h1", last - 1)
        take_roots(groups[last - 2])
        layer_one(last, 0)
        layer_one(last, 1, on_vector=True)
        square(groups[last - 1], 0)
        quantise_round("h1", last)
        add_eps(groups[last - 2])
        layer_two(last - 1, 0, shared)
        invert_norms(groups[last - 2])
        scale(groups[last - 2], nc.gpsimd)
        square(groups[last - 1], 1)
        layer_two(last - 1, 1, on_vector)
        take_roots(groups[last - 1])
        tile_a, tile_b = ((last - 1, 1),), ((last, 0),)
        square(tile_a, 0)
        add_eps(groups[last - 1])
        take_roots(tile_a)
        layer_two(last, 0, shared)
        invert_norms(groups[last - 1])
        scale(groups[last - 1], nc.gpsimd, nc.vector)
        square(tile_b, 0)
        add_eps(tile_a)
        layer_two(last, 1, on_vector)
        invert_norms(tile_a)
        scale(tile_a, nc.vector)
        take_roots(tile_b)
        square(groups[ROUNDS], 0)
        add_eps(tile_b)
        invert_norms(tile_b)
        scale(tile_b, nc.vector)
        take_roots(groups[ROUNDS])
        add_eps(groups[ROUNDS])
        invert_norms(groups[ROUNDS])
        scale_halves(groups[ROUNDS])
